import numpy as np
import ml_dtypes


def mxq(x, axis, fmt="e4m3"):
    dtype, down = {"e4m3": (ml_dtypes.float8_e4m3fn, 7), "e5m2": (ml_dtypes.float8_e5m2, 14)}[fmt]
    v = np.moveaxis(np.asarray(x, np.float32).astype(ml_dtypes.bfloat16).astype(np.float64), axis, -1)
    blocks = v.reshape(v.shape[:-1] + (-1, 32))
    amax = np.abs(blocks).max(-1, keepdims=True)
    byte = np.maximum(np.where(amax > 0, np.frexp(amax)[1] - 1 + 127, 0) - down, 1)
    scale = np.exp2(byte - 127.0)
    codes = (blocks / scale).astype(np.float32).astype(dtype).astype(np.float64)
    return np.moveaxis((codes * scale).reshape(v.shape), -1, axis)


WIDE = False


def mx_kscale(k):
    if not WIDE:
        return np.ones(k)
    levels = np.array([10, -10, 5, -5, 0])
    if k % 512:
        return np.exp2(np.random.permutation(np.resize(levels, k // 32))).repeat(32)
    a = np.empty((k // 512, 16))
    for p in range(k // 512):
        a[p, :8] = np.random.permutation(np.resize(levels, 8))
        for g in range(8):
            far = levels[np.abs(levels - a[p, g]) >= 10]
            a[p, g + 8] = far[np.random.randint(len(far))]
    return np.exp2(a.ravel()).repeat(32)


BF16 = ml_dtypes.bfloat16


def bf(x):
    return np.asarray(x, np.float32).astype(BF16)


def f64(x):
    return np.asarray(x).astype(np.float64)


B, S, IN, OUT, R = 4, 512, 1024, 1024, 8
T = B * S
CURV = 0.1
EPS = 1e-7


def lorentz_saved(x, z, a):
    sk = np.sqrt(CURV)
    xn = np.maximum(np.sqrt(np.sum(x * x, axis=-1, keepdims=True)), EPS)
    p_time = sk * np.cosh(xn / sk)
    p_space = (sk * np.sinh(xn / sk) / xn) * x
    zn = np.maximum(np.sqrt(np.sum(z * z, axis=-1)), EPS)
    inner = (p_space @ z.T) * np.cosh(sk * a) - p_time * (np.sinh(sk * a) * zn)
    return xn, sk * inner / zn


def setup_inputs():
    s = mx_kscale(T)
    s = (s / np.min(s)).reshape(B, S, 1)
    u = mx_kscale(OUT)
    w = np.random.standard_normal((R, IN))
    c = np.sqrt(3.0 / R)
    v = np.random.standard_normal((B, S, IN)) + c * (np.random.standard_normal((B, S, R)) @ w)
    length = np.random.uniform(0.4, 1.5, (B, S, 1))
    v = v / np.sqrt(np.sum(v * v, axis=-1, keepdims=True)) * length
    h = np.random.standard_normal((OUT, IN)) + c * (np.random.standard_normal((OUT, R)) @ w)
    h = h / np.sqrt(np.sum(h * h, axis=-1, keepdims=True)) * np.random.uniform(0.7, 1.4, (OUT, 1))
    x0 = bf(v)
    z0 = bf(h)
    a = bf(np.random.standard_normal(OUT))
    g = bf(np.random.standard_normal((B, S, OUT)) * np.exp2(np.random.randint(-6, 1, (B, S, 1))) / s * u)
    xn, q = lorentz_saved(f64(x0), f64(z0), f64(a))
    return {"x": bf(f64(x0) * s), "z": bf(f64(z0) / u[:, None]), "a": a, "xn": np.asarray(xn, np.float32), "q": np.asarray(q, np.float32), "grad_out": g}


def reference(x, z, a, xn, q, grad_out):
    sk = np.sqrt(CURV)
    x2 = f64(x).reshape(T, IN)
    z, a = f64(z), f64(a)
    n = f64(xn).reshape(T, 1)
    qq = f64(q).reshape(T, OUT)
    g = f64(grad_out).reshape(T, OUT)
    sh = np.sinh(n / sk)
    ch = np.cosh(n / sk)
    lam = sk * sh / n
    p_space = lam * x2
    e = x2 / np.sqrt(np.sum(x2 * x2, axis=1, keepdims=True))
    zn = np.sqrt(np.sum(z * z, axis=1))
    sa = np.sinh(sk * a)
    ca = np.cosh(sk * a)
    r = np.sqrt(1.0 + qq * qq)
    dd = g * (ca / r)
    dps = mxq(dd, 1, "e5m2") @ mxq(z, 0, "e4m3")
    m = mxq(dd, 0, "e5m2").T @ mxq(p_space, 0, "e4m3")
    gpt = -np.sum(g * (sa * zn / r), axis=1, keepdims=True)
    pe = np.sum(dps * e, axis=1, keepdims=True)
    dx = lam * dps + ((ch - lam) * pe + sh * gpt) * e
    cz = (np.arcsinh(qq) - qq / r) / sk - (sk * ch) * sa / r
    gzn = np.sum(g * cz, axis=0)
    dzw = m + (gzn / zn)[:, None] * z
    return dx.reshape(B, S, IN), dzw

@@ -1,0 +1,454 @@
+import math
+from contextlib import ExitStack
+
+import concourse.mybir as mybir
+from concourse.masks import make_identity
+
+F32 = mybir.dt.float32
+BF16 = mybir.dt.bfloat16
+U32 = mybir.dt.uint32
+U8 = mybir.dt.uint8
+I32 = mybir.dt.int32
+E4 = mybir.dt.float8_e4m3fn_x4
+E5 = mybir.dt.float8_e5m2_x4
+ALU = mybir.AluOpType
+ACT = mybir.ActivationFunctionType
+AX = mybir.AxisListType
+
+P = 128
+NG = 4
+NJ = 4
+OUT = 1024
+IN = 1024
+NB = OUT // P
+NGO = OUT // 512
+NH = IN // 512
+SK = math.sqrt(0.1)
+FLOPS = 2 * 2 * 2048 * 1024 * 1024
+
+
+def tile_lorentz_fully_connected_mlr_angle_v_kernel(tc, x, z, a, xn, q, grad_out, out_0, out_1):
+    nc = tc.nc
+    xv = x.rearrange("g (p j) i -> p g j i", j=NJ)
+    qv = q.rearrange("g (p j) o -> p g j o", j=NJ)
+    gv = grad_out.rearrange("g (p j) o -> p g j o", j=NJ)
+    o0v = out_0.rearrange("g (p j) i -> p g j i", j=NJ)
+    xnv = xn.rearrange("g (p j) one -> p g (j one)", j=NJ)
+    zkv = z.rearrange("(G p j) i -> p G j i", G=NGO, j=NJ)
+    znv = z.rearrange("(b m) i -> m b i", m=P)
+    o1v = out_1.rearrange("(b m) i -> m b i", m=P)
+
+    with ExitStack() as ctx:
+        ctx.enter_context(tc.manual_schedule())
+        keep = ctx.enter_context(tc.tile_pool(name="keep", bufs=1))
+        work = ctx.enter_context(tc.tile_pool(name="work", bufs=2))
+        psum = ctx.enter_context(tc.psum_pool(name="psum", bufs=1))
+
+        ident_f = keep.tile([P, P], F32, name="ident_f")
+        ident_b = keep.tile([P, P], BF16, name="ident_b")
+        ddt_c = keep.tile([P, NG, OUT], U32, name="ddt_c", align_bytes=64)
+        ddt_s = keep.tile([P, NG, OUT], U8, name="ddt_s", align_bytes=64)
+        ps_c = keep.tile([P, NG, IN], U32, name="ps_c", align_bytes=64)
+        ps_s = keep.tile([P, NG, IN], U8, name="ps_s", align_bytes=64)
+        z_c = keep.tile([P, NGO, IN], U32, name="z_c", align_bytes=64)
+        z_s = keep.tile([P, NGO, IN], U8, name="z_s", align_bytes=64)
+        ca_bc = keep.tile([P, OUT], F32, name="ca_bc")
+        c_bc = keep.tile([P, OUT], F32, name="c_bc")
+        qs_acc = keep.tile([P, NB, P], F32, name="qs_acc")
+        th_acc = keep.tile([P, 2, NB, 2], F32, name="th_acc")
+        junk_v = keep.tile([P, OUT], F32, name="junk_v")
+        junk_a = keep.tile([P, IN], BF16, name="junk_a")
+        one = keep.tile([P, 1], F32, name="one")
+        c2 = keep.tile([P, 2], F32, name="c2")
+        a_rows = keep.tile([P, P], BF16, name="a_rows")
+        a_mb = keep.tile([P, NB], F32, name="a_mb")
+        ea = keep.tile([P, NB], F32, name="ea")
+        eb = keep.tile([P, NB], F32, name="eb")
+        ca_mb = keep.tile([P, NB], F32, name="ca_mb")
+        sa_mb = keep.tile([P, NB], F32, name="sa_mb")
+        zn2 = keep.tile([P, NB], F32, name="zn2")
+        zn_mb = keep.tile([P, NB], F32, name="zn_mb")
+        izn = keep.tile([P, NB], F32, name="izn")
+        c_mb = keep.tile([P, NB], F32, name="c_mb")
+        xn_t = keep.tile([P, NG, NJ], F32, name="xn_t")
+        ep = keep.tile([P, NG, NJ], F32, name="ep")
+        em = keep.tile([P, NG, NJ], F32, name="em")
+        sh = keep.tile([P, NG, NJ], F32, name="sh")
+        ch = keep.tile([P, NG, NJ], F32, name="ch")
+        rxn = keep.tile([P, NG, NJ], F32, name="rxn")
+        lam = keep.tile([P, NG, NJ], F32, name="lam")
+        ilam = keep.tile([P, NG, NJ], F32, name="ilam")
+        t0 = keep.tile([P, NG, NJ], F32, name="t0")
+        chn = keep.tile([P, NG, NJ, 2], F32, name="chn")
+
+        qt, gt, xt, x1, x2, aq, sg, nat, grp = {}, {}, {}, {}, {}, {}, {}, {}, {}
+        trp, go, oc, osc, accp, yt, st = {}, {}, {}, {}, {}, {}, {}
+
+        for g in range(NG):
+            for nm in ("nx2", "nx", "inx", "inx2", "alpha", "beta", "gsum", "bg", "dpy", "coef"):
+                st[(nm, g)] = keep.tile([P, NJ], F32, name="%s%d" % (nm, g))
+
+        def load_q(g, j):
+            qt[(g, j)] = work.tile([P, OUT], F32, name="q", tag="q", bufs=5)
+            nc.sync.dma_start(out=qt[(g, j)][:], in_=qv[:, g, j, :])
+
+        def load_g(g, j):
+            gt[(g, j)] = work.tile([P, OUT], BF16, name="g", tag="g", bufs=5)
+            nc.sync.dma_start(out=gt[(g, j)][:], in_=gv[:, g, j, :])
+
+        def load_x(g, j):
+            xt[(g, j)] = work.tile([P, IN], BF16, name="x", tag="x", bufs=8)
+            nc.sync.dma_start(out=xt[(g, j)][:], in_=xv[:, g, j, :])
+
+        def sq(g, j):
+            x1[(g, j)] = work.tile([P, OUT], F32, name="x1", tag="x1", bufs=4)
+            nc.scalar.activation(out=x1[(g, j)][:], in_=qt[(g, j)][:], func=ACT.Square)
+
+        def sr(g, j):
+            x2[(g, j)] = work.tile([P, OUT], F32, name="x2", tag="x2", bufs=4)
+            nc.scalar.activation(out=x2[(g, j)][:], in_=x1[(g, j)][:], func=ACT.Sqrt, bias=one[:], scale=1.0)
+
+        def ar(g, j):
+            nc.scalar.activation(out=x1[(g, j)][:], in_=x1[(g, j)][:], func=ACT.Abs_reciprocal_sqrt, bias=one[:], scale=1.0)
+
+        def ln(g, j):
+            nc.scalar.activation(out=x2[(g, j)][:], in_=x2[(g, j)][:], func=ACT.Ln)
+
+        def ab(g, j):
+            aq[(g, j)] = work.tile([P, OUT], F32, name="aq", tag="aq", bufs=2)
+            nc.vector.tensor_scalar(out=aq[(g, j)][:].bitcast(I32), in0=qt[(g, j)][:].bitcast(I32), scalar1=0x7FFFFFFF, scalar2=None, op0=ALU.bitwise_and)
+
+        def s_add(g, j):
+            nc.vector.tensor_tensor(out=x2[(g, j)][:], in0=aq[(g, j)][:], in1=x2[(g, j)][:], op=ALU.add)
+
+        def sgn(g, j):
+            sg[(g, j)] = work.tile([P, OUT], BF16, name="sg", tag="sg", bufs=3)
+            nc.vector.tensor_scalar(out=sg[(g, j)][:], in0=qt[(g, j)][:], scalar1=0.0, scalar2=0.5, op0=ALU.is_ge, op1=ALU.subtract)
+
+        def b_mul(g, j):
+            nc.vector.tensor_tensor(out=x1[(g, j)][:], in0=gt[(g, j)][:], in1=x1[(g, j)][:], op=ALU.mult)
+
+        def dd_mul(g, j):
+            if j == 0:
+                nat[("d", g)] = work.tile([P, NJ, OUT], BF16, name="nat", tag="nat", bufs=2)
+            nc.vector.tensor_tensor(out=nat[("d", g)][:, j, :], in0=x1[(g, j)][:], in1=ca_bc[:], op=ALU.mult)
+
+        def gs_sum(g, j):
+            nc.vector.scalar_tensor_tensor(out=junk_v[:], in0=x1[(g, j)][:], scalar=1.0, in1=c_bc[:], op0=ALU.mult, op1=ALU.mult, accum_out=st[("gsum", g)][:, j : j + 1])
+
+        def gg(g, j):
+            nc.vector.tensor_tensor(out=gt[(g, j)][:], in0=gt[(g, j)][:], in1=sg[(g, j)][:], op=ALU.mult)
+
+        def ha(g, j):
+            nc.vector.tensor_tensor(out=x2[(g, j)][:], in0=gt[(g, j)][:], in1=x2[(g, j)][:], op=ALU.mult)
+
+        def tr(g, j):
+            trp[(g, j)] = psum.tile([P, NGO, 2, P], F32, name="tr", tag="tr", bufs=2)
+            words = nat[("d", g)][:, j, :].bitcast(F32)
+            for G in range(NGO):
+                for u in range(2):
+                    nc.tensor.transpose(out=trp[(g, j)][:, G, u, :], in_=words[:, 256 * G + u : 256 * (G + 1) : 2], identity=ident_f[:])
+
+        def te(g, j):
+            go[(g, j)] = work.tile([P, NGO * P * 4], BF16, name="go", tag="go", bufs=3, align_bytes=64)
+            nc.scalar.copy(out=go[(g, j)][:].bitcast(F32).rearrange("p (G r u) -> p G r u", G=NGO, u=2), in_=trp[(g, j)][:].rearrange("p G u r -> p G r u"))
+
+        def qo(g, j):
+            oc[(g, j)] = work.tile([P, NGO * P], U32, name="oc", tag="oc", bufs=5, align_bytes=64)
+            osc[(g, j)] = work.tile([P, NGO * P], U8, name="osc", tag="osc", bufs=5, align_bytes=64)
+            nc.vector.quantize_mx(out=oc[(g, j)][:].bitcast(E5), scales=osc[(g, j)][:], in_=go[(g, j)][:])
+
+        def mx(g, j):
+            for h in range(NH):
+                accp[(g, j, h)] = psum.tile([P, 512], F32, name="acc", tag="acc", bufs=3)
+                for G in range(NGO):
+                    nc.tensor.matmul_mx(out=accp[(g, j, h)][:], lhsT=oc[(g, j)][:, P * G : P * (G + 1)].bitcast(E5), lhsT_scale=osc[(g, j)][:, P * G : P * (G + 1)],
+                                        rhs=z_c[:, G, 512 * h : 512 * (h + 1)].bitcast(E4), rhs_scale=z_s[:, G, 512 * h : 512 * (h + 1)], start=(G == 0), stop=(G == NGO - 1))
+
+        def ye(g, j):
+            yt[(g, j)] = work.tile([P, IN], F32, name="y", tag="y", bufs=4)
+            for h in range(NH):
+                nc.scalar.activation(out=yt[(g, j)][:, 512 * h : 512 * (h + 1)], in_=accp[(g, j, h)][:], func=ACT.Copy, scale=lam[:, g, j : j + 1])
+
+        def pep(g, j):
+            nc.vector.scalar_tensor_tensor(out=junk_v[:], in0=yt[(g, j)][:], scalar=1.0, in1=xt[(g, j)][:], op0=ALU.mult, op1=ALU.mult, accum_out=st[("dpy", g)][:, j : j + 1])
+
+        def co(g, j):
+            nc.vector.scalar_tensor_tensor(out=st[("coef", g)][:, j : j + 1], in0=st[("dpy", g)][:, j : j + 1], scalar=st[("alpha", g)][:, j : j + 1], in1=st[("bg", g)][:, j : j + 1], op0=ALU.mult, op1=ALU.subtract)
+
+        def fi(g, j):
+            nc.vector.scalar_tensor_tensor(out=yt[(g, j)][:], in0=xt[(g, j)][:], scalar=st[("coef", g)][:, j : j + 1], in1=yt[(g, j)][:], op0=ALU.mult, op1=ALU.add)
+            nc.sync.dma_start(out=o0v[:, g, j, :], in_=yt[(g, j)][:])
+
+        def it(g):
+            grp[("d", g)] = work.tile([P, OUT, NJ], BF16, name="grp", tag="grp", bufs=1, align_bytes=64)
+            for k in range(2):
+                nc.scalar.copy(out=grp[("d", g)][:, 512 * k : 512 * (k + 1), :], in_=nat[("d", g)][:, :, 512 * k : 512 * (k + 1)].rearrange("p j w -> p w j"))
+
+        def qt_(g):
+            nc.vector.quantize_mx(out=ddt_c[:, g, :].bitcast(E5), scales=ddt_s[:, g, :], in_=grp[("d", g)][:].rearrange("p w j -> p (w j)"))
+
+        def ps(g, j):
+            if j == 0:
+                nat[("p", g)] = work.tile([P, NJ, IN], BF16, name="nat", tag="nat", bufs=2)
+            nc.scalar.activation(out=nat[("p", g)][:, j, :], in_=xt[(g, j)][:], func=ACT.Copy, scale=lam[:, g, j : j + 1])
+
+        def ip(g):
+            grp[("p", g)] = work.tile([P, IN, NJ], BF16, name="grp", tag="grp", bufs=1, align_bytes=64)
+            nc.vector.tensor_copy(out=grp[("p", g)][:], in_=nat[("p", g)][:].rearrange("p j w -> p w j"))
+
+        def qp(g):
+            nc.vector.quantize_mx(out=ps_c[:, g, :].bitcast(E4), scales=ps_s[:, g, :], in_=grp[("p", g)][:].rearrange("p w j -> p (w j)"))
+
+        def xx(g, j):
+            nc.scalar.activation(out=junk_a[:], in_=xt[(g, j)][:], func=ACT.Square, accum_out=st[("nx2", g)][:, j : j + 1])
+
+        def xx_v(g, j):
+            nc.vector.scalar_tensor_tensor(out=junk_v[:], in0=xt[(g, j)][:], scalar=1.0, in1=xt[(g, j)][:], op0=ALU.mult, op1=ALU.mult, accum_out=st[("nx2", g)][:, j : j + 1])
+
+        def nxs(g):
+            nc.scalar.activation(out=st[("nx", g)][:], in_=st[("nx2", g)][:], func=ACT.Sqrt)
+
+        def inx(g):
+            nc.vector.reciprocal(out=st[("inx", g)][:], in_=st[("nx", g)][:])
+            nc.vector.tensor_tensor(out=st[("beta", g)][:], in0=sh[:, g, :], in1=st[("inx", g)][:], op=ALU.mult)
+            nc.vector.tensor_tensor(out=st[("inx2", g)][:], in0=st[("inx", g)][:], in1=st[("inx", g)][:], op=ALU.mult)
+            nc.vector.tensor_tensor(out=st[("alpha", g)][:], in0=t0[:, g, :], in1=st[("inx2", g)][:], op=ALU.mult)
+
+        def bg(g):
+            nc.vector.tensor_tensor(out=st[("bg", g)][:], in0=st[("beta", g)][:], in1=st[("gsum", g)][:], op=ALU.mult)
+
+        def qf(g):
+            trp[("th", g)] = psum.tile([P, 2, NB, 2], F32, name="th", tag="th", bufs=1)
+            for b in range(NB):
+                if b % 4 == 0:
+                    trp[("qs", g, b // 4)] = psum.tile([P, 4, P], F32, name="qs", tag="qs", bufs=2)
+                cols = slice(P * b, P * (b + 1))
+                for j in range(NJ):
+                    nc.tensor.matmul(out=trp[("qs", g, b // 4)][:, b % 4, :], lhsT=x1[(g, j)][:, cols], rhs=qt[(g, j)][:, cols], start=(j == 0), stop=(j == NJ - 1))
+                    nc.tensor.matmul(out=trp[("th", g)][:, 0, b, :], lhsT=x1[(g, j)][:, cols], rhs=chn[:, g, j, :], start=(j == 0), stop=(j == NJ - 1))
+
+        def hf(g, b0, b1):
+            for b in range(b0, b1):
+                for j in range(NJ):
+                    nc.tensor.matmul(out=trp[("th", g)][:, 1, b, :], lhsT=x2[(g, j)][:, P * b : P * (b + 1)], rhs=c2[:], start=(j == 0), stop=(j == NJ - 1))
+
+        def qse(g):
+            for k in range(2):
+                nc.vector.tensor_tensor(out=qs_acc[:, 4 * k : 4 * (k + 1), :], in0=trp[("qs", g, k)][:], in1=qs_acc[:, 4 * k : 4 * (k + 1), :], op=ALU.add)
+
+        def the(g):
+            nc.vector.tensor_tensor(out=th_acc[:], in0=trp[("th", g)][:], in1=th_acc[:], op=ALU.add)
+
+        def bcast(vec, dst):
+            for k in range(2):
+                bc = psum.tile([P, 4, P], F32, name="acc", tag="acc", bufs=3)
+                for b in range(4):
+                    nc.tensor.matmul(out=bc[:, b, :], lhsT=vec[:, 4 * k + b : 4 * k + b + 1].to_broadcast([P, P]), rhs=ident_f[:], start=True, stop=True)
+                nc.vector.tensor_copy(out=dst[:, 512 * k : 512 * (k + 1)], in_=bc[:].rearrange("p b n -> p (b n)"))
+
+        make_identity(nc, ident_b[:])
+        make_identity(nc, ident_f[:])
+        nc.vector.memset(a_rows[:], 0.0)
+        nc.vector.memset(one[:], 1.0)
+        nc.vector.memset(c2[:], 1.0)
+        nc.vector.memset(qs_acc[:], 0.0)
+        nc.vector.memset(th_acc[:], 0.0)
+        nc.sync.dma_start(out=xn_t[:], in_=xnv)
+        nc.sync.dma_start(out=a_rows[0:NB, :], in_=a.rearrange("(b m) -> b m", m=P))
+        for j in range(NJ):
+            load_q(0, j)
+            load_g(0, j)
+        zt = {}
+        for b in range(NB):
+            zt[b] = work.tile([P, IN], BF16, name="x", tag="x", bufs=8)
+            nc.sync.dma_start(out=zt[b][:], in_=znv[:, b, :])
+
+        nc.scalar.activation(out=ep[:], in_=xn_t[:], func=ACT.Exp, scale=1.0 / SK)
+        nc.scalar.activation(out=em[:], in_=xn_t[:], func=ACT.Exp, scale=-1.0 / SK)
+        at_ps = psum.tile([P, P], BF16, name="tr", tag="tr", bufs=2)
+        nc.tensor.transpose(out=at_ps[:], in_=a_rows[:], identity=ident_b[:])
+        nc.vector.tensor_copy(out=a_mb[:], in_=at_ps[:, 0:NB])
+        nc.scalar.activation(out=ea[:], in_=a_mb[:], func=ACT.Exp, scale=SK)
+        nc.scalar.activation(out=eb[:], in_=a_mb[:], func=ACT.Exp, scale=-SK)
+        for j in range(NJ):
+            sq(0, j)
+        nc.vector.tensor_tensor(out=ca_mb[:], in0=ea[:], in1=eb[:], op=ALU.add)
+        nc.vector.tensor_tensor(out=sa_mb[:], in0=ea[:], in1=eb[:], op=ALU.subtract)
+        nc.vector.tensor_scalar(out=ca_mb[:], in0=ca_mb[:], scalar1=0.5, scalar2=None, op0=ALU.mult)
+        nc.vector.tensor_scalar(out=sa_mb[:], in0=sa_mb[:], scalar1=0.5, scalar2=None, op0=ALU.mult)
+        bcast(ca_mb, ca_bc)
+        nc.vector.tensor_tensor(out=sh[:], in0=ep[:], in1=em[:], op=ALU.subtract)
+        nc.vector.tensor_tensor(out=ch[:], in0=ep[:], in1=em[:], op=ALU.add)
+        nc.vector.reciprocal(out=rxn[:], in_=xn_t[:])
+        nc.vector.tensor_scalar(out=sh[:], in0=sh[:], scalar1=0.5, scalar2=None, op0=ALU.mult)
+        nc.vector.tensor_scalar(out=ch[:], in0=ch[:], scalar1=0.5, scalar2=None, op0=ALU.mult)
+        nc.vector.scalar_tensor_tensor(out=lam[:], in0=sh[:], scalar=SK, in1=rxn[:], op0=ALU.mult, op1=ALU.mult)
+        nc.vector.tensor_scalar(out=chn[:], in0=ch[:].unsqueeze(3).to_broadcast([P, NG, NJ, 2]), scalar1=-SK, scalar2=None, op0=ALU.mult)
+        nc.vector.reciprocal(out=ilam[:], in_=lam[:])
+        nc.vector.tensor_tensor(out=t0[:], in0=ch[:], in1=ilam[:], op=ALU.mult)
+        nc.vector.tensor_scalar(out=t0[:], in0=t0[:], scalar1=-1.0, scalar2=None, op0=ALU.add)
+
+        def z_sq(b):
+            nc.vector.scalar_tensor_tensor(out=junk_v[:], in0=zt[b][:], scalar=1.0, in1=zt[b][:], op0=ALU.mult, op1=ALU.mult, accum_out=zn2[:, b : b + 1])
+
+        def z_codes():
+            for G in range(NGO):
+                grp[("z", G)] = work.tile([P, IN, NJ], BF16, name="grp", tag="grp", bufs=1, align_bytes=64)
+                nc.vector.tensor_copy(out=grp[("z", G)][:], in_=nat[("z", G)][:].rearrange("p j w -> p w j"))
+                nc.vector.quantize_mx(out=z_c[:, G, :].bitcast(E4), scales=z_s[:, G, :], in_=grp[("z", G)][:].rearrange("p w j -> p (w j)"))
+
+        def epi(g, js):
+            for j in js:
+                pep(g, j)
+            for j in js:
+                co(g, j)
+            for j in js:
+                fi(g, j)
+
+        for g in range(NG):
+            more = g + 1 < NG
+            for j in range(NJ):
+                sr(g, j)
+            if g > 0:
+                nxs(g)
+                qse(g - 1)
+                the(g - 1)
+                epi(g - 1, (2, 3))
+            if more and g > 0:
+                for j in range(NJ):
+                    load_x(g + 1, j)
+                load_q(g + 1, 0)
+                load_g(g + 1, 0)
+            if not more:
+                for b in range(4):
+                    zt[b] = work.tile([P, IN], BF16, name="x", tag="x", bufs=8)
+                    nc.sync.dma_start(out=zt[b][:], in_=znv[:, b, :])
+            ab(g, 0)
+            ab(g, 1)
+            s_add(g, 0)
+            ab(g, 2)
+            s_add(g, 1)
+            ab(g, 3)
+            s_add(g, 2)
+            s_add(g, 3)
+            for j in range(NJ):
+                ar(g, j)
+            if g > 0:
+                inx(g)
+            else:
+                for b in range(4):
+                    z_sq(b)
+            for j in range(NJ):
+                ln(g, j)
+            b_mul(g, 0)
+            b_mul(g, 1)
+            dd_mul(g, 0)
+            tr(g, 0)
+            b_mul(g, 2)
+            dd_mul(g, 1)
+            tr(g, 1)
+            b_mul(g, 3)
+            dd_mul(g, 2)
+            dd_mul(g, 3)
+            if g == 0:
+                for b in range(4, NB):
+                    z_sq(b)
+                for j in range(NJ):
+                    load_x(0, j)
+                for G in range(NGO):
+                    nat[("z", G)] = work.tile([P, NJ, IN], BF16, name="natz", tag="natz", bufs=2)
+                    nc.sync.dma_start(out=nat[("z", G)][:], in_=zkv[:, G, :, :])
+                for j in range(NJ):
+                    load_x(1, j)
+                load_q(1, 0)
+                load_g(1, 0)
+                nc.scalar.activation(out=zn_mb[:], in_=zn2[:], func=ACT.Sqrt)
+                for j in range(NJ):
+                    xx_v(0, j)
+                nxs(0)
+                nc.vector.reciprocal(out=izn[:], in_=zn_mb[:])
+                nc.vector.tensor_tensor(out=c_mb[:], in0=sa_mb[:], in1=zn_mb[:], op=ALU.mult)
+                bcast(c_mb, c_bc)
+                inx(0)
+            te(g, 0)
+            tr(g, 2)
+            te(g, 1)
+            tr(g, 3)
+            if g == 0:
+                z_codes()
+            if more:
+                xx(g + 1, 0)
+            te(g, 2)
+            if more:
+                xx(g + 1, 1)
+            qo(g, 0)
+            te(g, 3)
+            gs_sum(g, 0)
+            for j in range(1, NJ):
+                qo(g, j)
+                gs_sum(g, j)
+            bg(g)
+            qf(g)
+            it(g)
+            sgn(g, 0)
+            sgn(g, 1)
+            gg(g, 0)
+            sgn(g, 2)
+            gg(g, 1)
+            sgn(g, 3)
+            gg(g, 2)
+            gg(g, 3)
+            if more:
+                for j in range(1, NJ):
+                    load_q(g + 1, j)
+            for j in range(NJ):
+                ha(g, j)
+            if more:
+                for j in range(1, NJ):
+                    load_g(g + 1, j)
+            qt_(g)
+            for j in range(NJ):
+                ps(g, j)
+            ip(g)
+            if more:
+                xx(g + 1, 2)
+                xx(g + 1, 3)
+            mx(g, 0)
+            ye(g, 0)
+            qp(g)
+            for j in range(1, NJ):
+                hf(g, 2 * j - 2, 2 * j)
+                mx(g, j)
+                ye(g, j)
+            hf(g, 6, 8)
+            if more:
+                for j in range(NJ):
+                    sq(g + 1, j)
+            epi(g, (0, 1))
+
+        dg = work.tile([P, NB, P], F32, name="aq", tag="aq", bufs=2)
+        s1b = keep.tile([P, NB], F32, name="s1b")
+        gz = keep.tile([P, NB], F32, name="gz")
+        so = keep.tile([P, NB], F32, name="so")
+        qse(NG - 1)
+        the(NG - 1)
+        nc.vector.tensor_tensor(out=dg[:], in0=qs_acc[:], in1=ident_f[:].unsqueeze(1).to_broadcast([P, NB, P]), op=ALU.mult)
+        nc.vector.tensor_tensor(out=gz[:], in0=sa_mb[:], in1=th_acc[:, 0, :, 0], op=ALU.mult)
+        nc.vector.tensor_reduce(out=s1b[:], in_=dg[:], axis=AX.X, op=ALU.add)
+        nc.vector.scalar_tensor_tensor(out=gz[:], in0=th_acc[:, 1, :, 0], scalar=2.0 / SK, in1=gz[:], op0=ALU.mult, op1=ALU.add)
+        nc.vector.scalar_tensor_tensor(out=gz[:], in0=s1b[:], scalar=-1.0 / SK, in1=gz[:], op0=ALU.mult, op1=ALU.add)
+        nc.vector.tensor_tensor(out=so[:], in0=gz[:], in1=izn[:], op=ALU.mult)
+        epi(NG - 1, (2, 3))
+        for b in range(4, NB):
+            zt[b] = work.tile([P, IN], BF16, name="x", tag="x", bufs=8)
+            nc.sync.dma_start(out=zt[b][:], in_=znv[:, b, :])
+        for b in range(NB):
+            o1 = work.tile([P, IN], F32, name="y", tag="y", bufs=4)
+            for h in range(NH):
+                macc = psum.tile([P, 512], F32, name="acc", tag="acc", bufs=3)
+                for g in range(NG):
+                    nc.tensor.matmul_mx(out=macc[:], lhsT=ddt_c[:, g, P * b : P * (b + 1)].bitcast(E5), lhsT_scale=ddt_s[:, g, P * b : P * (b + 1)],
+                                        rhs=ps_c[:, g, 512 * h : 512 * (h + 1)].bitcast(E4), rhs_scale=ps_s[:, g, 512 * h : 512 * (h + 1)], start=(g == 0), stop=(g == NG - 1))
+                nc.vector.scalar_tensor_tensor(out=o1[:, 512 * h : 512 * (h + 1)], in0=zt[b][:, 512 * h : 512 * (h + 1)], scalar=so[:, b : b + 1], in1=macc[:], op0=ALU.mult, op1=ALU.add)
+            nc.sync.dma_start(out=o1v[:, b, :], in_=o1[:])

@@ -23,8 +23,11 @@ IN = 1024
 NB = OUT // P
 NGO = OUT // 512
 NH = IN // 512
+QW = 136
+QN = 130
 SK = math.sqrt(0.1)
 FLOPS = 2 * 2 * 2048 * 1024 * 1024
+M_BANKS = (("acc", 3), ("acc", 3), ("acc", 3), ("tr", 2), ("tr", 2), ("qs", 2), ("qs", 2))
 
 
 def tile_lorentz_fully_connected_mlr_angle_v_kernel(tc, x, z, a, xn, q, grad_out, out_0, out_1):
@@ -54,8 +57,7 @@ def tile_lorentz_fully_connected_mlr_angle_v_kernel(tc, x, z, a, xn, q, grad_out
         z_s = keep.tile([P, NGO, IN], U8, name="z_s", align_bytes=64)
         ca_bc = keep.tile([P, OUT], F32, name="ca_bc")
         c_bc = keep.tile([P, OUT], F32, name="c_bc")
-        qs_acc = keep.tile([P, NB, P], F32, name="qs_acc")
-        th_acc = keep.tile([P, 2, NB, 2], F32, name="th_acc")
+        qs_acc = keep.tile([P, NB * QN + 2 * NB * NJ], F32, name="qs_acc")
         junk_v = keep.tile([P, OUT], F32, name="junk_v")
         junk_a = keep.tile([P, IN], BF16, name="junk_a")
         one = keep.tile([P, 1], F32, name="one")
@@ -89,8 +91,14 @@ def tile_lorentz_fully_connected_mlr_angle_v_kernel(tc, x, z, a, xn, q, grad_out
                 st[(nm, g)] = keep.tile([P, NJ], F32, name="%s%d" % (nm, g))
 
         def load_q(g, j):
-            qt[(g, j)] = work.tile([P, OUT], F32, name="q", tag="q", bufs=5)
-            nc.sync.dma_start(out=qt[(g, j)][:], in_=qv[:, g, j, :])
+            qt[(g, j)] = work.tile([P, NB, QW], F32, name="q", tag="q", bufs=5)
+            nc.sync.dma_start(out=qt[(g, j)][:, :, 0:P], in_=qv[:, g, j, :].rearrange("p (b n) -> p b n", n=P))
+
+        def put_ch(g, j):
+            nc.gpsimd.tensor_copy(out=qt[(g, j)][:, :, P:QN], in_=chn[:, g, j, :].unsqueeze(1).to_broadcast([P, NB, 2]))
+
+        def blocks(t):
+            return t[:].rearrange("p (b n) -> p b n", n=P)
 
         def load_g(g, j):
             gt[(g, j)] = work.tile([P, OUT], BF16, name="g", tag="g", bufs=5)
@@ -102,7 +110,7 @@ def tile_lorentz_fully_connected_mlr_angle_v_kernel(tc, x, z, a, xn, q, grad_out
 
         def sq(g, j):
             x1[(g, j)] = work.tile([P, OUT], F32, name="x1", tag="x1", bufs=4)
-            nc.scalar.activation(out=x1[(g, j)][:], in_=qt[(g, j)][:], func=ACT.Square)
+            nc.scalar.activation(out=blocks(x1[(g, j)]), in_=qt[(g, j)][:, :, 0:P], func=ACT.Square)
 
         def sr(g, j):
             x2[(g, j)] = work.tile([P, OUT], F32, name="x2", tag="x2", bufs=4)
@@ -116,14 +124,14 @@ def tile_lorentz_fully_connected_mlr_angle_v_kernel(tc, x, z, a, xn, q, grad_out
 
         def ab(g, j):
             aq[(g, j)] = work.tile([P, OUT], F32, name="aq", tag="aq", bufs=2)
-            nc.vector.tensor_scalar(out=aq[(g, j)][:].bitcast(I32), in0=qt[(g, j)][:].bitcast(I32), scalar1=0x7FFFFFFF, scalar2=None, op0=ALU.bitwise_and)
+            nc.vector.tensor_scalar(out=blocks(aq[(g, j)]).bitcast(I32), in0=qt[(g, j)][:, :, 0:P].bitcast(I32), scalar1=0x7FFFFFFF, scalar2=None, op0=ALU.bitwise_and)
 
         def s_add(g, j):
             nc.vector.tensor_tensor(out=x2[(g, j)][:], in0=aq[(g, j)][:], in1=x2[(g, j)][:], op=ALU.add)
 
         def sgn(g, j):
             sg[(g, j)] = work.tile([P, OUT], BF16, name="sg", tag="sg", bufs=3)
-            nc.vector.tensor_scalar(out=sg[(g, j)][:], in0=qt[(g, j)][:], scalar1=0.0, scalar2=0.5, op0=ALU.is_ge, op1=ALU.subtract)
+            nc.vector.tensor_scalar(out=blocks(sg[(g, j)]), in0=qt[(g, j)][:, :, 0:P], scalar1=0.0, scalar2=0.5, op0=ALU.is_ge, op1=ALU.subtract)
 
         def b_mul(g, j):
             nc.vector.tensor_tensor(out=x1[(g, j)][:], in0=gt[(g, j)][:], in1=x1[(g, j)][:], op=ALU.mult)
@@ -218,34 +226,36 @@ def tile_lorentz_fully_connected_mlr_angle_v_kernel(tc, x, z, a, xn, q, grad_out
         def bg(g):
             nc.vector.tensor_tensor(out=st[("bg", g)][:], in0=st[("beta", g)][:], in1=st[("gsum", g)][:], op=ALU.mult)
 
-        def qf(g):
-            trp[("th", g)] = psum.tile([P, 2, NB, 2], F32, name="th", tag="th", bufs=1)
-            for b in range(NB):
-                if b % 4 == 0:
-                    trp[("qs", g, b // 4)] = psum.tile([P, 4, P], F32, name="qs", tag="qs", bufs=2)
-                cols = slice(P * b, P * (b + 1))
-                for j in range(NJ):
-                    nc.tensor.matmul(out=trp[("qs", g, b // 4)][:, b % 4, :], lhsT=x1[(g, j)][:, cols], rhs=qt[(g, j)][:, cols], start=(j == 0), stop=(j == NJ - 1))
-                    nc.tensor.matmul(out=trp[("th", g)][:, 0, b, :], lhsT=x1[(g, j)][:, cols], rhs=chn[:, g, j, :], start=(j == 0), stop=(j == NJ - 1))
-
-        def hf(g, b0, b1):
+        def qf(g, b0, b1):
             for b in range(b0, b1):
+                if b in (0, 3):
+                    trp[("s", g, b // 3)] = psum.tile([P, 3 * QN], F32, name="qs", tag="qs", bufs=2)
+                if b == 6:
+                    trp[("s", g, 2)] = psum.tile([P, 2 * QN + 2 * NB * NJ], F32, name="th", tag="th", bufs=1)
                 for j in range(NJ):
-                    nc.tensor.matmul(out=trp[("th", g)][:, 1, b, :], lhsT=x2[(g, j)][:, P * b : P * (b + 1)], rhs=c2[:], start=(j == 0), stop=(j == NJ - 1))
+                    nc.tensor.matmul(out=trp[("s", g, b // 3)][:, QN * (b % 3) : QN * (b % 3 + 1)], lhsT=x1[(g, j)][:, P * b : P * (b + 1)], rhs=qt[(g, j)][:, b, 0:QN], start=(j == 0), stop=(j == NJ - 1))
+
+        def hf(g, j):
+            for b in range(NB):
+                c0 = 2 * QN + 2 * (NB * j + b)
+                nc.tensor.matmul(out=trp[("s", g, 2)][:, c0 : c0 + 2], lhsT=x2[(g, j)][:, P * b : P * (b + 1)], rhs=c2[:], start=True, stop=True)
 
         def qse(g):
             for k in range(2):
-                nc.vector.tensor_tensor(out=qs_acc[:, 4 * k : 4 * (k + 1), :], in0=trp[("qs", g, k)][:], in1=qs_acc[:, 4 * k : 4 * (k + 1), :], op=ALU.add)
+                nc.vector.tensor_tensor(out=qs_acc[:, 3 * QN * k : 3 * QN * (k + 1)], in0=trp[("s", g, k)][:], in1=qs_acc[:, 3 * QN * k : 3 * QN * (k + 1)], op=ALU.add)
 
         def the(g):
-            nc.vector.tensor_tensor(out=th_acc[:], in0=trp[("th", g)][:], in1=th_acc[:], op=ALU.add)
+            nc.vector.tensor_tensor(out=qs_acc[:, 6 * QN :], in0=trp[("s", g, 2)][:], in1=qs_acc[:, 6 * QN :], op=ALU.add)
 
-        def bcast(vec, dst):
+        def bcast(vec, nm, tag, bufs):
             for k in range(2):
-                bc = psum.tile([P, 4, P], F32, name="acc", tag="acc", bufs=3)
+                trp[(nm, k)] = psum.tile([P, 4, P], F32, name=tag, tag=tag, bufs=bufs)
                 for b in range(4):
-                    nc.tensor.matmul(out=bc[:, b, :], lhsT=vec[:, 4 * k + b : 4 * k + b + 1].to_broadcast([P, P]), rhs=ident_f[:], start=True, stop=True)
-                nc.vector.tensor_copy(out=dst[:, 512 * k : 512 * (k + 1)], in_=bc[:].rearrange("p b n -> p (b n)"))
+                    nc.tensor.matmul(out=trp[(nm, k)][:, b, :], lhsT=vec[:, 4 * k + b : 4 * k + b + 1].to_broadcast([P, P]), rhs=ident_f[:], start=True, stop=True)
+
+        def bcast_out(nm, dst):
+            for k in range(2):
+                nc.vector.tensor_copy(out=dst[:, 512 * k : 512 * (k + 1)], in_=trp[(nm, k)][:].rearrange("p b n -> p (b n)"))
 
         make_identity(nc, ident_b[:])
         make_identity(nc, ident_f[:])
@@ -253,16 +263,18 @@ def tile_lorentz_fully_connected_mlr_angle_v_kernel(tc, x, z, a, xn, q, grad_out
         nc.vector.memset(one[:], 1.0)
         nc.vector.memset(c2[:], 1.0)
         nc.vector.memset(qs_acc[:], 0.0)
-        nc.vector.memset(th_acc[:], 0.0)
         nc.sync.dma_start(out=xn_t[:], in_=xnv)
         nc.sync.dma_start(out=a_rows[0:NB, :], in_=a.rearrange("(b m) -> b m", m=P))
         for j in range(NJ):
             load_q(0, j)
+        for G in range(NGO):
+            nat[("z", G)] = work.tile([P, NJ, IN], BF16, name="natz", tag="natz", bufs=2)
+            nc.sync.dma_start(out=nat[("z", G)][:], in_=zkv[:, G, :, :])
+        for j in range(NJ):
             load_g(0, j)
+        for j in range(NJ):
+            load_x(0, j)
         zt = {}
-        for b in range(NB):
-            zt[b] = work.tile([P, IN], BF16, name="x", tag="x", bufs=8)
-            nc.sync.dma_start(out=zt[b][:], in_=znv[:, b, :])
 
         nc.scalar.activation(out=ep[:], in_=xn_t[:], func=ACT.Exp, scale=1.0 / SK)
         nc.scalar.activation(out=em[:], in_=xn_t[:], func=ACT.Exp, scale=-1.0 / SK)
@@ -273,30 +285,39 @@ def tile_lorentz_fully_connected_mlr_angle_v_kernel(tc, x, z, a, xn, q, grad_out
         nc.scalar.activation(out=eb[:], in_=a_mb[:], func=ACT.Exp, scale=-SK)
         for j in range(NJ):
             sq(0, j)
+            sr(0, j)
+        nc.vector.tensor_tensor(out=ch[:], in0=ep[:], in1=em[:], op=ALU.add)
+        nc.vector.tensor_tensor(out=sh[:], in0=ep[:], in1=em[:], op=ALU.subtract)
+        nc.vector.tensor_scalar(out=chn[:], in0=ch[:].unsqueeze(3).to_broadcast([P, NG, NJ, 2]), scalar1=-0.5 * SK, scalar2=None, op0=ALU.mult)
+        for j in range(NJ):
+            put_ch(0, j)
         nc.vector.tensor_tensor(out=ca_mb[:], in0=ea[:], in1=eb[:], op=ALU.add)
         nc.vector.tensor_tensor(out=sa_mb[:], in0=ea[:], in1=eb[:], op=ALU.subtract)
         nc.vector.tensor_scalar(out=ca_mb[:], in0=ca_mb[:], scalar1=0.5, scalar2=None, op0=ALU.mult)
         nc.vector.tensor_scalar(out=sa_mb[:], in0=sa_mb[:], scalar1=0.5, scalar2=None, op0=ALU.mult)
-        bcast(ca_mb, ca_bc)
-        nc.vector.tensor_tensor(out=sh[:], in0=ep[:], in1=em[:], op=ALU.subtract)
-        nc.vector.tensor_tensor(out=ch[:], in0=ep[:], in1=em[:], op=ALU.add)
+        bcast(ca_mb, "ca", "acc", 3)
         nc.vector.reciprocal(out=rxn[:], in_=xn_t[:])
         nc.vector.tensor_scalar(out=sh[:], in0=sh[:], scalar1=0.5, scalar2=None, op0=ALU.mult)
         nc.vector.tensor_scalar(out=ch[:], in0=ch[:], scalar1=0.5, scalar2=None, op0=ALU.mult)
         nc.vector.scalar_tensor_tensor(out=lam[:], in0=sh[:], scalar=SK, in1=rxn[:], op0=ALU.mult, op1=ALU.mult)
-        nc.vector.tensor_scalar(out=chn[:], in0=ch[:].unsqueeze(3).to_broadcast([P, NG, NJ, 2]), scalar1=-SK, scalar2=None, op0=ALU.mult)
         nc.vector.reciprocal(out=ilam[:], in_=lam[:])
         nc.vector.tensor_tensor(out=t0[:], in0=ch[:], in1=ilam[:], op=ALU.mult)
         nc.vector.tensor_scalar(out=t0[:], in0=t0[:], scalar1=-1.0, scalar2=None, op0=ALU.add)
 
-        def z_sq(b):
-            nc.vector.scalar_tensor_tensor(out=junk_v[:], in0=zt[b][:], scalar=1.0, in1=zt[b][:], op0=ALU.mult, op1=ALU.mult, accum_out=zn2[:, b : b + 1])
+        def load_zrows(k):
+            nat[("r", k)] = work.tile([P, 4, IN], BF16, name="natz", tag="natz", bufs=2)
+            nc.sync.dma_start(out=nat[("r", k)][:], in_=znv[:, 4 * k : 4 * (k + 1), :])
 
-        def z_codes():
-            for G in range(NGO):
-                grp[("z", G)] = work.tile([P, IN, NJ], BF16, name="grp", tag="grp", bufs=1, align_bytes=64)
-                nc.vector.tensor_copy(out=grp[("z", G)][:], in_=nat[("z", G)][:].rearrange("p j w -> p w j"))
-                nc.vector.quantize_mx(out=z_c[:, G, :].bitcast(E4), scales=z_s[:, G, :], in_=grp[("z", G)][:].rearrange("p w j -> p (w j)"))
+        def z_sq(b):
+            rows = nat[("r", b // 4)][:, b % 4, :]
+            nc.vector.scalar_tensor_tensor(out=junk_v[:], in0=rows, scalar=1.0, in1=rows, op0=ALU.mult, op1=ALU.mult, accum_out=zn2[:, b : b + 1])
+
+        def z_codes(G):
+            grp[("z", G)] = work.tile([P, IN, NJ], BF16, name="grp", tag="grp", bufs=1, align_bytes=64)
+            nc.vector.tensor_copy(out=grp[("z", G)][:], in_=nat[("z", G)][:].rearrange("p j w -> p w j"))
+
+        def z_quant(G):
+            nc.vector.quantize_mx(out=z_c[:, G, :].bitcast(E4), scales=z_s[:, G, :], in_=grp[("z", G)][:].rearrange("p w j -> p (w j)"))
 
         def epi(g, js):
             for j in js:
@@ -306,91 +327,121 @@ def tile_lorentz_fully_connected_mlr_angle_v_kernel(tc, x, z, a, xn, q, grad_out
             for j in js:
                 fi(g, j)
 
+        def m_out(b):
+            o1 = work.tile([P, IN], F32, name="y", tag="y", bufs=4)
+            for h in range(NH):
+                tag, bufs = M_BANKS[(NH * b + h) % len(M_BANKS)]
+                macc = psum.tile([P, 512], F32, name=tag, tag=tag, bufs=bufs)
+                for g in range(NG):
+                    nc.tensor.matmul_mx(out=macc[:], lhsT=ddt_c[:, g, P * b : P * (b + 1)].bitcast(E5), lhsT_scale=ddt_s[:, g, P * b : P * (b + 1)],
+                                        rhs=ps_c[:, g, 512 * h : 512 * (h + 1)].bitcast(E4), rhs_scale=ps_s[:, g, 512 * h : 512 * (h + 1)], start=(g == 0), stop=(g == NG - 1))
+                nc.vector.scalar_tensor_tensor(out=o1[:, 512 * h : 512 * (h + 1)], in0=zt[b][:, 512 * h : 512 * (h + 1)], scalar=so[:, b : b + 1], in1=macc[:], op0=ALU.mult, op1=ALU.add)
+            nc.sync.dma_start(out=o1v[:, b, :], in_=o1[:])
+
+        def load_z(b):
+            zt[b] = work.tile([P, IN], BF16, name="x", tag="x", bufs=8)
+            nc.sync.dma_start(out=zt[b][:], in_=znv[:, b, :])
+
         for g in range(NG):
             more = g + 1 < NG
-            for j in range(NJ):
-                sr(g, j)
             if g > 0:
+                for j in range(NJ):
+                    sr(g, j)
                 nxs(g)
                 qse(g - 1)
-                the(g - 1)
                 epi(g - 1, (2, 3))
-            if more and g > 0:
-                for j in range(NJ):
-                    load_x(g + 1, j)
-                load_q(g + 1, 0)
-                load_g(g + 1, 0)
-            if not more:
-                for b in range(4):
-                    zt[b] = work.tile([P, IN], BF16, name="x", tag="x", bufs=8)
-                    nc.sync.dma_start(out=zt[b][:], in_=znv[:, b, :])
+                if more:
+                    for j in range(NJ):
+                        load_x(g + 1, j)
+                    load_q(g + 1, 0)
+                    put_ch(g + 1, 0)
+                    load_g(g + 1, 0)
+                else:
+                    for b in range(4):
+                        load_z(b)
             ab(g, 0)
             ab(g, 1)
             s_add(g, 0)
+            if g == 0:
+                z_codes(0)
+                load_zrows(0)
             ab(g, 2)
             s_add(g, 1)
+            if g == 0:
+                z_quant(0)
             ab(g, 3)
             s_add(g, 2)
-            s_add(g, 3)
-            for j in range(NJ):
-                ar(g, j)
-            if g > 0:
-                inx(g)
-            else:
-                for b in range(4):
-                    z_sq(b)
-            for j in range(NJ):
-                ln(g, j)
-            b_mul(g, 0)
-            b_mul(g, 1)
-            dd_mul(g, 0)
-            tr(g, 0)
-            b_mul(g, 2)
-            dd_mul(g, 1)
-            tr(g, 1)
-            b_mul(g, 3)
-            dd_mul(g, 2)
-            dd_mul(g, 3)
             if g == 0:
-                for b in range(4, NB):
-                    z_sq(b)
-                for j in range(NJ):
-                    load_x(0, j)
-                for G in range(NGO):
-                    nat[("z", G)] = work.tile([P, NJ, IN], BF16, name="natz", tag="natz", bufs=2)
-                    nc.sync.dma_start(out=nat[("z", G)][:], in_=zkv[:, G, :, :])
+                z_codes(1)
+                load_zrows(1)
                 for j in range(NJ):
                     load_x(1, j)
                 load_q(1, 0)
+                put_ch(1, 0)
                 load_g(1, 0)
-                nc.scalar.activation(out=zn_mb[:], in_=zn2[:], func=ACT.Sqrt)
+            s_add(g, 3)
+            if g == 0:
+                z_quant(1)
+            for j in range(NJ):
+                ar(g, j)
+            if g > 0:
+                the(g - 1)
+                inx(g)
+            else:
+                bcast_out("ca", ca_bc)
+            for j in range(NJ):
+                ln(g, j)
+            if g > 0:
                 for j in range(NJ):
-                    xx_v(0, j)
-                nxs(0)
-                nc.vector.reciprocal(out=izn[:], in_=zn_mb[:])
-                nc.vector.tensor_tensor(out=c_mb[:], in0=sa_mb[:], in1=zn_mb[:], op=ALU.mult)
-                bcast(c_mb, c_bc)
-                inx(0)
+                    ps(g, j)
+            else:
+                for j in range(NJ):
+                    xx(0, j)
+            for j in range(NJ):
+                b_mul(g, j)
+            qf(g, 0, 3)
+            dd_mul(g, 0)
+            tr(g, 0)
+            dd_mul(g, 1)
+            tr(g, 1)
+            dd_mul(g, 2)
+            dd_mul(g, 3)
             te(g, 0)
             tr(g, 2)
             te(g, 1)
             tr(g, 3)
-            if g == 0:
-                z_codes()
-            if more:
-                xx(g + 1, 0)
+            qf(g, 3, 8)
+            if g > 0:
+                ip(g)
+            else:
+                for b in range(3):
+                    z_sq(b)
             te(g, 2)
-            if more:
-                xx(g + 1, 1)
             qo(g, 0)
             te(g, 3)
-            gs_sum(g, 0)
-            for j in range(1, NJ):
-                qo(g, j)
-                gs_sum(g, j)
-            bg(g)
-            qf(g)
-            it(g)
+            if g == 0:
+                z_sq(3)
+                qo(g, 1)
+                z_sq(4)
+                qo(g, 2)
+                z_sq(5)
+                qo(g, 3)
+                z_sq(6)
+                z_sq(7)
+                it(g)
+                nc.scalar.activation(out=zn_mb[:], in_=zn2[:], func=ACT.Sqrt)
+                nxs(0)
+            else:
+                gs_sum(g, 0)
+                qp(g)
+                for j in range(1, NJ):
+                    qo(g, j)
+                    gs_sum(g, j)
+                bg(g)
+                it(g)
+            for j in range(NJ):
+                mx(g, j)
+                ye(g, j)
             sgn(g, 0)
             sgn(g, 1)
             gg(g, 0)
@@ -402,53 +453,63 @@ def tile_lorentz_fully_connected_mlr_angle_v_kernel(tc, x, z, a, xn, q, grad_out
             if more:
                 for j in range(1, NJ):
                     load_q(g + 1, j)
+                    put_ch(g + 1, j)
+            if g == 0:
+                nc.vector.reciprocal(out=izn[:], in_=zn_mb[:])
+                nc.vector.tensor_tensor(out=c_mb[:], in0=sa_mb[:], in1=zn_mb[:], op=ALU.mult)
+                bcast(c_mb, "c", "tr", 2)
             for j in range(NJ):
                 ha(g, j)
+                hf(g, j)
             if more:
                 for j in range(1, NJ):
                     load_g(g + 1, j)
             qt_(g)
-            for j in range(NJ):
-                ps(g, j)
-            ip(g)
-            if more:
-                xx(g + 1, 2)
-                xx(g + 1, 3)
-            mx(g, 0)
-            ye(g, 0)
-            qp(g)
-            for j in range(1, NJ):
-                hf(g, 2 * j - 2, 2 * j)
-                mx(g, j)
-                ye(g, j)
-            hf(g, 6, 8)
+            if g == 0:
+                for j in range(NJ):
+                    ps(g, j)
+                bcast_out("c", c_bc)
+                for j in range(NJ):
+                    gs_sum(g, j)
+                inx(0)
+                ip(g)
+                bg(g)
+                qp(g)
             if more:
                 for j in range(NJ):
+                    xx(g + 1, j)
+                for j in range(NJ):
                     sq(g + 1, j)
-            epi(g, (0, 1))
+                epi(g, (0, 1))
 
+        g = NG - 1
         dg = work.tile([P, NB, P], F32, name="aq", tag="aq", bufs=2)
         s1b = keep.tile([P, NB], F32, name="s1b")
+        hs = keep.tile([P, NB], F32, name="hs")
         gz = keep.tile([P, NB], F32, name="gz")
         so = keep.tile([P, NB], F32, name="so")
-        qse(NG - 1)
-        the(NG - 1)
-        nc.vector.tensor_tensor(out=dg[:], in0=qs_acc[:], in1=ident_f[:].unsqueeze(1).to_broadcast([P, NB, P]), op=ALU.mult)
-        nc.vector.tensor_tensor(out=gz[:], in0=sa_mb[:], in1=th_acc[:, 0, :, 0], op=ALU.mult)
+        sums = qs_acc[:, 0 : NB * QN].rearrange("p (b n) -> p b n", n=QN)
+        hsum = qs_acc[:, NB * QN :].rearrange("p (j b two) -> p b two j", j=NJ, two=2)
+        qse(g)
+        for j in range(NJ):
+            pep(g, j)
+        the(g)
+        for j in range(NJ):
+            co(g, j)
+        nc.vector.tensor_tensor(out=dg[:], in0=sums[:, :, 0:P], in1=ident_f[:].unsqueeze(1).to_broadcast([P, NB, P]), op=ALU.mult)
+        nc.vector.tensor_reduce(out=hs[:], in_=hsum[:, :, 0, :], axis=AX.X, op=ALU.add)
+        nc.vector.tensor_tensor(out=gz[:], in0=sa_mb[:], in1=sums[:, :, P], op=ALU.mult)
         nc.vector.tensor_reduce(out=s1b[:], in_=dg[:], axis=AX.X, op=ALU.add)
-        nc.vector.scalar_tensor_tensor(out=gz[:], in0=th_acc[:, 1, :, 0], scalar=2.0 / SK, in1=gz[:], op0=ALU.mult, op1=ALU.add)
+        nc.vector.scalar_tensor_tensor(out=gz[:], in0=hs[:], scalar=2.0 / SK, in1=gz[:], op0=ALU.mult, op1=ALU.add)
+        fi(g, 0)
         nc.vector.scalar_tensor_tensor(out=gz[:], in0=s1b[:], scalar=-1.0 / SK, in1=gz[:], op0=ALU.mult, op1=ALU.add)
+        fi(g, 1)
         nc.vector.tensor_tensor(out=so[:], in0=gz[:], in1=izn[:], op=ALU.mult)
-        epi(NG - 1, (2, 3))
-        for b in range(4, NB):
-            zt[b] = work.tile([P, IN], BF16, name="x", tag="x", bufs=8)
-            nc.sync.dma_start(out=zt[b][:], in_=znv[:, b, :])
+        load_z(4)
+        load_z(5)
+        fi(g, 2)
+        fi(g, 3)
+        load_z(6)
+        load_z(7)
         for b in range(NB):
-            o1 = work.tile([P, IN], F32, name="y", tag="y", bufs=4)
-            for h in range(NH):
-                macc = psum.tile([P, 512], F32, name="acc", tag="acc", bufs=3)
-                for g in range(NG):
-                    nc.tensor.matmul_mx(out=macc[:], lhsT=ddt_c[:, g, P * b : P * (b + 1)].bitcast(E5), lhsT_scale=ddt_s[:, g, P * b : P * (b + 1)],
-                                        rhs=ps_c[:, g, 512 * h : 512 * (h + 1)].bitcast(E4), rhs_scale=ps_s[:, g, 512 * h : 512 * (h + 1)], start=(g == 0), stop=(g == NG - 1))
-                nc.vector.scalar_tensor_tensor(out=o1[:, 512 * h : 512 * (h + 1)], in0=zt[b][:, 512 * h : 512 * (h + 1)], scalar=so[:, b : b + 1], in1=macc[:], op0=ALU.mult, op1=ALU.add)
-            nc.sync.dma_start(out=o1v[:, b, :], in_=o1[:])
+            m_out(b)

@@ -57,11 +57,11 @@ def tile_lorentz_fully_connected_mlr_angle_v_kernel(tc, x, z, a, xn, q, grad_out
         z_s = keep.tile([P, NGO, IN], U8, name="z_s", align_bytes=64)
         ca_bc = keep.tile([P, OUT], F32, name="ca_bc")
         c_bc = keep.tile([P, OUT], F32, name="c_bc")
-        qs_acc = keep.tile([P, NB * QN + 2 * NB * NJ], F32, name="qs_acc")
+        qs_acc = keep.tile([P, NB * QN], F32, name="qs_acc")
+        hpart = keep.tile([P, NG, NB], F32, name="hpart")
         junk_v = keep.tile([P, OUT], F32, name="junk_v")
         junk_a = keep.tile([P, IN], BF16, name="junk_a")
         one = keep.tile([P, 1], F32, name="one")
-        c2 = keep.tile([P, 2], F32, name="c2")
         a_rows = keep.tile([P, P], BF16, name="a_rows")
         a_mb = keep.tile([P, NB], F32, name="a_mb")
         ea = keep.tile([P, NB], F32, name="ea")
@@ -123,15 +123,20 @@ def tile_lorentz_fully_connected_mlr_angle_v_kernel(tc, x, z, a, xn, q, grad_out
             nc.scalar.activation(out=x2[(g, j)][:], in_=x2[(g, j)][:], func=ACT.Ln)
 
         def ab(g, j):
-            aq[(g, j)] = work.tile([P, OUT], F32, name="aq", tag="aq", bufs=2)
-            nc.vector.tensor_scalar(out=blocks(aq[(g, j)]).bitcast(I32), in0=qt[(g, j)][:, :, 0:P].bitcast(I32), scalar1=0x7FFFFFFF, scalar2=None, op0=ALU.bitwise_and)
+            if g == 0:
+                aq[(g, j)] = work.tile([P, OUT], F32, name="y", tag="y", bufs=5)[:]
+            else:
+                if j % 2 == 0:
+                    aq[("pair", g, j // 2)] = work.tile([P, 2, OUT], F32, name="natz", tag="natz", bufs=2)
+                aq[(g, j)] = aq[("pair", g, j // 2)][:, j % 2, :]
+            nc.scalar.activation(out=aq[(g, j)].rearrange("p (b n) -> p b n", n=P), in_=qt[(g, j)][:, :, 0:P], func=ACT.Abs)
 
         def s_add(g, j):
-            nc.vector.tensor_tensor(out=x2[(g, j)][:], in0=aq[(g, j)][:], in1=x2[(g, j)][:], op=ALU.add)
+            nc.vector.tensor_tensor(out=x2[(g, j)][:], in0=aq[(g, j)], in1=x2[(g, j)][:], op=ALU.add)
 
         def sgn(g, j):
-            sg[(g, j)] = work.tile([P, OUT], BF16, name="sg", tag="sg", bufs=3)
-            nc.vector.tensor_scalar(out=blocks(sg[(g, j)]), in0=qt[(g, j)][:, :, 0:P], scalar1=0.0, scalar2=0.5, op0=ALU.is_ge, op1=ALU.subtract)
+            sg[(g, j)] = work.tile([P, OUT], BF16, name="sg", tag="sg", bufs=4)
+            nc.scalar.activation(out=blocks(sg[(g, j)]), in_=qt[(g, j)][:, :, 0:P], func=ACT.Sign)
 
         def b_mul(g, j):
             nc.vector.tensor_tensor(out=x1[(g, j)][:], in0=gt[(g, j)][:], in1=x1[(g, j)][:], op=ALU.mult)
@@ -174,7 +179,7 @@ def tile_lorentz_fully_connected_mlr_angle_v_kernel(tc, x, z, a, xn, q, grad_out
                                         rhs=z_c[:, G, 512 * h : 512 * (h + 1)].bitcast(E4), rhs_scale=z_s[:, G, 512 * h : 512 * (h + 1)], start=(G == 0), stop=(G == NGO - 1))
 
         def ye(g, j):
-            yt[(g, j)] = work.tile([P, IN], F32, name="y", tag="y", bufs=4)
+            yt[(g, j)] = work.tile([P, IN], F32, name="y", tag="y", bufs=5)
             for h in range(NH):
                 nc.scalar.activation(out=yt[(g, j)][:, 512 * h : 512 * (h + 1)], in_=accp[(g, j, h)][:], func=ACT.Copy, scale=lam[:, g, j : j + 1])
 
@@ -190,8 +195,7 @@ def tile_lorentz_fully_connected_mlr_angle_v_kernel(tc, x, z, a, xn, q, grad_out
 
         def it(g):
             grp[("d", g)] = work.tile([P, OUT, NJ], BF16, name="grp", tag="grp", bufs=1, align_bytes=64)
-            for k in range(2):
-                nc.scalar.copy(out=grp[("d", g)][:, 512 * k : 512 * (k + 1), :], in_=nat[("d", g)][:, :, 512 * k : 512 * (k + 1)].rearrange("p j w -> p w j"))
+            nc.vector.tensor_copy(out=grp[("d", g)][:], in_=nat[("d", g)][:].rearrange("p j w -> p w j"))
 
         def qt_(g):
             nc.vector.quantize_mx(out=ddt_c[:, g, :].bitcast(E5), scales=ddt_s[:, g, :], in_=grp[("d", g)][:].rearrange("p w j -> p (w j)"))
@@ -199,7 +203,7 @@ def tile_lorentz_fully_connected_mlr_angle_v_kernel(tc, x, z, a, xn, q, grad_out
         def ps(g, j):
             if j == 0:
                 nat[("p", g)] = work.tile([P, NJ, IN], BF16, name="nat", tag="nat", bufs=2)
-            nc.scalar.activation(out=nat[("p", g)][:, j, :], in_=xt[(g, j)][:], func=ACT.Copy, scale=lam[:, g, j : j + 1])
+            nc.vector.tensor_scalar(out=nat[("p", g)][:, j, :], in0=xt[(g, j)][:], scalar1=lam[:, g, j : j + 1], scalar2=None, op0=ALU.mult)
 
         def ip(g):
             grp[("p", g)] = work.tile([P, IN, NJ], BF16, name="grp", tag="grp", bufs=1, align_bytes=64)
@@ -231,14 +235,18 @@ def tile_lorentz_fully_connected_mlr_angle_v_kernel(tc, x, z, a, xn, q, grad_out
                 if b in (0, 3):
                     trp[("s", g, b // 3)] = psum.tile([P, 3 * QN], F32, name="qs", tag="qs", bufs=2)
                 if b == 6:
-                    trp[("s", g, 2)] = psum.tile([P, 2 * QN + 2 * NB * NJ], F32, name="th", tag="th", bufs=1)
+                    trp[("s", g, 2)] = psum.tile([P, 2 * QN], F32, name="th", tag="th", bufs=1)
                 for j in range(NJ):
                     nc.tensor.matmul(out=trp[("s", g, b // 3)][:, QN * (b % 3) : QN * (b % 3 + 1)], lhsT=x1[(g, j)][:, P * b : P * (b + 1)], rhs=qt[(g, j)][:, b, 0:QN], start=(j == 0), stop=(j == NJ - 1))
 
-        def hf(g, j):
-            for b in range(NB):
-                c0 = 2 * QN + 2 * (NB * j + b)
-                nc.tensor.matmul(out=trp[("s", g, 2)][:, c0 : c0 + 2], lhsT=x2[(g, j)][:, P * b : P * (b + 1)], rhs=c2[:], start=True, stop=True)
+        def hf(g):
+            for k in range(2):
+                ht = psum.tile([P, 4, P], F32, name="tr", tag="tr", bufs=2)
+                for b in range(4):
+                    for j in range(NJ):
+                        nc.tensor.matmul(out=ht[:, b, :], lhsT=x2[(g, j)][:, P * (4 * k + b) : P * (4 * k + b + 1)], rhs=ident_f[:], is_transpose=True, start=(j == 0), stop=(j == NJ - 1))
+                for b in range(4):
+                    nc.scalar.activation(out=junk_a[:, 0:P], in_=ht[:, b, :], func=ACT.Copy, accum_out=hpart[:, g, 4 * k + b : 4 * k + b + 1])
 
         def qse(g):
             for k in range(2):
@@ -261,10 +269,12 @@ def tile_lorentz_fully_connected_mlr_angle_v_kernel(tc, x, z, a, xn, q, grad_out
         make_identity(nc, ident_f[:])
         nc.vector.memset(a_rows[:], 0.0)
         nc.vector.memset(one[:], 1.0)
-        nc.vector.memset(c2[:], 1.0)
         nc.vector.memset(qs_acc[:], 0.0)
         nc.sync.dma_start(out=xn_t[:], in_=xnv)
         nc.sync.dma_start(out=a_rows[0:NB, :], in_=a.rearrange("(b m) -> b m", m=P))
+        for k in range(2):
+            nat[("r", k)] = work.tile([P, 4, IN], BF16, name="nat", tag="nat", bufs=2)
+            nc.sync.dma_start(out=nat[("r", k)][:], in_=znv[:, 4 * k : 4 * (k + 1), :])
         for j in range(NJ):
             load_q(0, j)
         for G in range(NGO):
@@ -283,9 +293,15 @@ def tile_lorentz_fully_connected_mlr_angle_v_kernel(tc, x, z, a, xn, q, grad_out
         nc.vector.tensor_copy(out=a_mb[:], in_=at_ps[:, 0:NB])
         nc.scalar.activation(out=ea[:], in_=a_mb[:], func=ACT.Exp, scale=SK)
         nc.scalar.activation(out=eb[:], in_=a_mb[:], func=ACT.Exp, scale=-SK)
+        for b in range(NB):
+            rows = nat[("r", b // 4)][:, b % 4, :]
+            nc.vector.scalar_tensor_tensor(out=junk_v[:], in0=rows, scalar=1.0, in1=rows, op0=ALU.mult, op1=ALU.mult, accum_out=zn2[:, b : b + 1])
         for j in range(NJ):
             sq(0, j)
+            ab(0, j)
             sr(0, j)
+            if j == 1:
+                nc.scalar.activation(out=zn_mb[:], in_=zn2[:], func=ACT.Sqrt)
         nc.vector.tensor_tensor(out=ch[:], in0=ep[:], in1=em[:], op=ALU.add)
         nc.vector.tensor_tensor(out=sh[:], in0=ep[:], in1=em[:], op=ALU.subtract)
         nc.vector.tensor_scalar(out=chn[:], in0=ch[:].unsqueeze(3).to_broadcast([P, NG, NJ, 2]), scalar1=-0.5 * SK, scalar2=None, op0=ALU.mult)
@@ -304,13 +320,6 @@ def tile_lorentz_fully_connected_mlr_angle_v_kernel(tc, x, z, a, xn, q, grad_out
         nc.vector.tensor_tensor(out=t0[:], in0=ch[:], in1=ilam[:], op=ALU.mult)
         nc.vector.tensor_scalar(out=t0[:], in0=t0[:], scalar1=-1.0, scalar2=None, op0=ALU.add)
 
-        def load_zrows(k):
-            nat[("r", k)] = work.tile([P, 4, IN], BF16, name="natz", tag="natz", bufs=2)
-            nc.sync.dma_start(out=nat[("r", k)][:], in_=znv[:, 4 * k : 4 * (k + 1), :])
-
-        def z_sq(b):
-            rows = nat[("r", b // 4)][:, b % 4, :]
-            nc.vector.scalar_tensor_tensor(out=junk_v[:], in0=rows, scalar=1.0, in1=rows, op0=ALU.mult, op1=ALU.mult, accum_out=zn2[:, b : b + 1])
 
         def z_codes(G):
             grp[("z", G)] = work.tile([P, IN, NJ], BF16, name="grp", tag="grp", bufs=1, align_bytes=64)
@@ -328,7 +337,7 @@ def tile_lorentz_fully_connected_mlr_angle_v_kernel(tc, x, z, a, xn, q, grad_out
                 fi(g, j)
 
         def m_out(b):
-            o1 = work.tile([P, IN], F32, name="y", tag="y", bufs=4)
+            o1 = work.tile([P, IN], F32, name="y", tag="y", bufs=5)
             for h in range(NH):
                 tag, bufs = M_BANKS[(NH * b + h) % len(M_BANKS)]
                 macc = psum.tile([P, 512], F32, name=tag, tag=tag, bufs=bufs)
@@ -359,21 +368,18 @@ def tile_lorentz_fully_connected_mlr_angle_v_kernel(tc, x, z, a, xn, q, grad_out
                 else:
                     for b in range(4):
                         load_z(b)
-            ab(g, 0)
-            ab(g, 1)
             s_add(g, 0)
             if g == 0:
                 z_codes(0)
-                load_zrows(0)
-            ab(g, 2)
             s_add(g, 1)
             if g == 0:
+                nc.vector.reciprocal(out=izn[:], in_=zn_mb[:])
+                nc.vector.tensor_tensor(out=c_mb[:], in0=sa_mb[:], in1=zn_mb[:], op=ALU.mult)
+                bcast(c_mb, "c", "tr", 2)
                 z_quant(0)
-            ab(g, 3)
             s_add(g, 2)
             if g == 0:
                 z_codes(1)
-                load_zrows(1)
                 for j in range(NJ):
                     load_x(1, j)
                 load_q(1, 0)
@@ -389,14 +395,13 @@ def tile_lorentz_fully_connected_mlr_angle_v_kernel(tc, x, z, a, xn, q, grad_out
                 inx(g)
             else:
                 bcast_out("ca", ca_bc)
+                bcast_out("c", c_bc)
+            for j in range(NJ):
+                ps(g, j)
             for j in range(NJ):
                 ln(g, j)
-            if g > 0:
-                for j in range(NJ):
-                    ps(g, j)
-            else:
-                for j in range(NJ):
-                    xx(0, j)
+            for j in range(NJ):
+                sgn(g, j)
             for j in range(NJ):
                 b_mul(g, j)
             qf(g, 0, 3)
@@ -411,85 +416,60 @@ def tile_lorentz_fully_connected_mlr_angle_v_kernel(tc, x, z, a, xn, q, grad_out
             te(g, 1)
             tr(g, 3)
             qf(g, 3, 8)
-            if g > 0:
-                ip(g)
-            else:
-                for b in range(3):
-                    z_sq(b)
+            ip(g)
             te(g, 2)
             qo(g, 0)
             te(g, 3)
             if g == 0:
-                z_sq(3)
-                qo(g, 1)
-                z_sq(4)
-                qo(g, 2)
-                z_sq(5)
-                qo(g, 3)
-                z_sq(6)
-                z_sq(7)
-                it(g)
-                nc.scalar.activation(out=zn_mb[:], in_=zn2[:], func=ACT.Sqrt)
+                for j in range(NJ):
+                    xx(0, j)
                 nxs(0)
-            else:
-                gs_sum(g, 0)
-                qp(g)
-                for j in range(1, NJ):
-                    qo(g, j)
-                    gs_sum(g, j)
-                bg(g)
-                it(g)
+            gs_sum(g, 0)
+            qp(g)
+            qo(g, 1)
+            gs_sum(g, 1)
+            it(g)
+            qo(g, 2)
+            gs_sum(g, 2)
+            qt_(g)
+            qo(g, 3)
+            gs_sum(g, 3)
+            if g == 0:
+                inx(0)
+            bg(g)
+            if more:
+                for j in range(NJ):
+                    xx(g + 1, j)
             for j in range(NJ):
                 mx(g, j)
                 ye(g, j)
-            sgn(g, 0)
-            sgn(g, 1)
-            gg(g, 0)
-            sgn(g, 2)
-            gg(g, 1)
-            sgn(g, 3)
-            gg(g, 2)
-            gg(g, 3)
+            for j in range(NJ):
+                gg(g, j)
             if more:
                 for j in range(1, NJ):
                     load_q(g + 1, j)
                     put_ch(g + 1, j)
-            if g == 0:
-                nc.vector.reciprocal(out=izn[:], in_=zn_mb[:])
-                nc.vector.tensor_tensor(out=c_mb[:], in0=sa_mb[:], in1=zn_mb[:], op=ALU.mult)
-                bcast(c_mb, "c", "tr", 2)
             for j in range(NJ):
                 ha(g, j)
-                hf(g, j)
             if more:
                 for j in range(1, NJ):
                     load_g(g + 1, j)
-            qt_(g)
-            if g == 0:
-                for j in range(NJ):
-                    ps(g, j)
-                bcast_out("c", c_bc)
-                for j in range(NJ):
-                    gs_sum(g, j)
-                inx(0)
-                ip(g)
-                bg(g)
-                qp(g)
             if more:
                 for j in range(NJ):
-                    xx(g + 1, j)
-                for j in range(NJ):
                     sq(g + 1, j)
+                for j in range(NJ):
+                    ab(g + 1, j)
+                hf(g)
                 epi(g, (0, 1))
 
         g = NG - 1
-        dg = work.tile([P, NB, P], F32, name="aq", tag="aq", bufs=2)
+        dg = work.tile([P, NB, P], F32, name="natz", tag="natz", bufs=2)
         s1b = keep.tile([P, NB], F32, name="s1b")
         hs = keep.tile([P, NB], F32, name="hs")
         gz = keep.tile([P, NB], F32, name="gz")
         so = keep.tile([P, NB], F32, name="so")
         sums = qs_acc[:, 0 : NB * QN].rearrange("p (b n) -> p b n", n=QN)
-        hsum = qs_acc[:, NB * QN :].rearrange("p (j b two) -> p b two j", j=NJ, two=2)
+        hf(g)
         qse(g)
         for j in range(NJ):
             pep(g, j)
@@ -497,10 +477,10 @@ def tile_lorentz_fully_connected_mlr_angle_v_kernel(tc, x, z, a, xn, q, grad_out
         for j in range(NJ):
             co(g, j)
         nc.vector.tensor_tensor(out=dg[:], in0=sums[:, :, 0:P], in1=ident_f[:].unsqueeze(1).to_broadcast([P, NB, P]), op=ALU.mult)
-        nc.vector.tensor_reduce(out=hs[:], in_=hsum[:, :, 0, :], axis=AX.X, op=ALU.add)
+        nc.vector.tensor_reduce(out=hs[:], in_=hpart[:].rearrange("p g b -> p b g"), axis=AX.X, op=ALU.add)
         nc.vector.tensor_tensor(out=gz[:], in0=sa_mb[:], in1=sums[:, :, P], op=ALU.mult)
         nc.vector.tensor_reduce(out=s1b[:], in_=dg[:], axis=AX.X, op=ALU.add)
-        nc.vector.scalar_tensor_tensor(out=gz[:], in0=hs[:], scalar=2.0 / SK, in1=gz[:], op0=ALU.mult, op1=ALU.add)
+        nc.vector.scalar_tensor_tensor(out=gz[:], in0=hs[:], scalar=1.0 / SK, in1=gz[:], op0=ALU.mult, op1=ALU.add)
         fi(g, 0)
         nc.vector.scalar_tensor_tensor(out=gz[:], in0=s1b[:], scalar=-1.0 / SK, in1=gz[:], op0=ALU.mult, op1=ALU.add)
         fi(g, 1)

@@ -27,7 +27,7 @@ QW = 136
 QN = 130
 SK = math.sqrt(0.1)
 FLOPS = 2 * 2 * 2048 * 1024 * 1024
-M_BANKS = (("acc", 3), ("acc", 3), ("acc", 3), ("tr", 2), ("tr", 2), ("qs", 2), ("qs", 2))
+M_BANKS = (("tr", 2), ("tr", 2), ("qs", 2), ("qs", 2), ("gt", 1))
 
 
 def tile_lorentz_fully_connected_mlr_angle_v_kernel(tc, x, z, a, xn, q, grad_out, out_0, out_1):
@@ -42,7 +42,6 @@ def tile_lorentz_fully_connected_mlr_angle_v_kernel(tc, x, z, a, xn, q, grad_out
     o1v = out_1.rearrange("(b m) i -> m b i", m=P)
 
     with ExitStack() as ctx:
-        ctx.enter_context(tc.manual_schedule())
         keep = ctx.enter_context(tc.tile_pool(name="keep", bufs=1))
         work = ctx.enter_context(tc.tile_pool(name="work", bufs=2))
         psum = ctx.enter_context(tc.psum_pool(name="psum", bufs=1))
@@ -84,11 +83,11 @@ def tile_lorentz_fully_connected_mlr_angle_v_kernel(tc, x, z, a, xn, q, grad_out
         chn = keep.tile([P, NG, NJ, 2], F32, name="chn")
 
         qt, gt, xt, x1, x2, aq, sg, nat, grp = {}, {}, {}, {}, {}, {}, {}, {}, {}
-        trp, go, oc, osc, accp, yt, st = {}, {}, {}, {}, {}, {}, {}
+        trp, go, oc, osc, accp, yt, st_, lt = {}, {}, {}, {}, {}, {}, {}, {}
 
         for g in range(NG):
             for nm in ("nx2", "nx", "inx", "inx2", "alpha", "beta", "gsum", "bg", "dpy", "coef"):
-                st[(nm, g)] = keep.tile([P, NJ], F32, name="%s%d" % (nm, g))
+                st_[(nm, g)] = keep.tile([P, NJ], F32, name="%s%d" % (nm, g))
 
         def load_q(g, j):
             qt[(g, j)] = work.tile([P, NB, QW], F32, name="q", tag="q", bufs=5)
@@ -119,20 +118,14 @@ def tile_lorentz_fully_connected_mlr_angle_v_kernel(tc, x, z, a, xn, q, grad_out
         def ar(g, j):
             nc.scalar.activation(out=x1[(g, j)][:], in_=x1[(g, j)][:], func=ACT.Abs_reciprocal_sqrt, bias=one[:], scale=1.0)
 
-        def ln(g, j):
-            nc.scalar.activation(out=x2[(g, j)][:], in_=x2[(g, j)][:], func=ACT.Ln)
-
         def ab(g, j):
             if g == 0:
-                aq[(g, j)] = work.tile([P, OUT], F32, name="y", tag="y", bufs=5)[:]
+                aq[(g, j)] = work.tile([P, OUT], F32, name="y", tag="y", bufs=4)[:]
             else:
                 if j % 2 == 0:
                     aq[("pair", g, j // 2)] = work.tile([P, 2, OUT], F32, name="natz", tag="natz", bufs=2)
                 aq[(g, j)] = aq[("pair", g, j // 2)][:, j % 2, :]
             nc.scalar.activation(out=aq[(g, j)].rearrange("p (b n) -> p b n", n=P), in_=qt[(g, j)][:, :, 0:P], func=ACT.Abs)
-
-        def s_add(g, j):
-            nc.vector.tensor_tensor(out=x2[(g, j)][:], in0=aq[(g, j)], in1=x2[(g, j)][:], op=ALU.add)
 
         def sgn(g, j):
             sg[(g, j)] = work.tile([P, OUT], BF16, name="sg", tag="sg", bufs=4)
@@ -147,13 +140,31 @@ def tile_lorentz_fully_connected_mlr_angle_v_kernel(tc, x, z, a, xn, q, grad_out
             nc.vector.tensor_tensor(out=nat[("d", g)][:, j, :], in0=x1[(g, j)][:], in1=ca_bc[:], op=ALU.mult)
 
         def gs_sum(g, j):
-            nc.vector.scalar_tensor_tensor(out=junk_v[:], in0=x1[(g, j)][:], scalar=1.0, in1=c_bc[:], op0=ALU.mult, op1=ALU.mult, accum_out=st[("gsum", g)][:, j : j + 1])
+            nc.vector.scalar_tensor_tensor(out=junk_v[:], in0=x1[(g, j)][:], scalar=1.0, in1=c_bc[:], op0=ALU.mult, op1=ALU.mult, accum_out=st_[("gsum", g)][:, j : j + 1])
 
         def gg(g, j):
-            nc.vector.tensor_tensor(out=gt[(g, j)][:], in0=gt[(g, j)][:], in1=sg[(g, j)][:], op=ALU.mult)
+            nc.vector.tensor_tensor(out=sg[(g, j)][:], in0=gt[(g, j)][:], in1=sg[(g, j)][:], op=ALU.mult)
 
-        def ha(g, j):
-            nc.vector.tensor_tensor(out=x2[(g, j)][:], in0=gt[(g, j)][:], in1=x2[(g, j)][:], op=ALU.mult)
+        def st(g, b):
+            tag = ("tr", "tr", "acc", "acc")[b % 4]
+            trp[("st", g, b)] = psum.tile([P, NJ, P], F32, name=tag, tag=tag, bufs=2)
+            cols = slice(P * b, P * (b + 1))
+            for j in range(NJ):
+                nc.tensor.matmul(out=trp[("st", g, b)][:, j, :], lhsT=aq[(g, j)][:, cols], rhs=ident_f[:], is_transpose=True, start=True, stop=False)
+                nc.tensor.matmul(out=trp[("st", g, b)][:, j, :], lhsT=x2[(g, j)][:, cols], rhs=ident_f[:], is_transpose=True, start=False, stop=True)
+
+        def ln_t(g, b):
+            lt[(g, b)] = work.tile([P, NJ * P], F32, name="lt", tag="lt", bufs=4)
+            nc.scalar.activation(out=lt[(g, b)][:], in_=trp[("st", g, b)][:].rearrange("p j t -> p (j t)"), func=ACT.Ln)
+
+        def g_t(g, k):
+            trp[("gt", g, k)] = psum.tile([P, 2, NJ, P], BF16, name="gt", tag="gt", bufs=1)
+            for b in (2 * k, 2 * k + 1):
+                for j in range(NJ):
+                    nc.tensor.transpose(out=trp[("gt", g, k)][:, b % 2, j, :], in_=sg[(g, j)][:, P * b : P * (b + 1)], identity=ident_b[:])
+
+        def hs_(g, b):
+            nc.vector.scalar_tensor_tensor(out=junk_v[:, 0 : NJ * P], in0=trp[("gt", g, b // 2)][:, b % 2, :, :].rearrange("p j t -> p (j t)"), scalar=1.0, in1=lt[(g, b)][:], op0=ALU.mult, op1=ALU.mult, accum_out=hpart[:, g, b : b + 1])
 
         def tr(g, j):
             trp[(g, j)] = psum.tile([P, NGO, 2, P], F32, name="tr", tag="tr", bufs=2)
@@ -173,24 +184,24 @@ def tile_lorentz_fully_connected_mlr_angle_v_kernel(tc, x, z, a, xn, q, grad_out
 
         def mx(g, j):
             for h in range(NH):
-                accp[(g, j, h)] = psum.tile([P, 512], F32, name="acc", tag="acc", bufs=3)
+                accp[(g, j, h)] = psum.tile([P, 512], F32, name="acc", tag="acc", bufs=2)
                 for G in range(NGO):
                     nc.tensor.matmul_mx(out=accp[(g, j, h)][:], lhsT=oc[(g, j)][:, P * G : P * (G + 1)].bitcast(E5), lhsT_scale=osc[(g, j)][:, P * G : P * (G + 1)],
                                         rhs=z_c[:, G, 512 * h : 512 * (h + 1)].bitcast(E4), rhs_scale=z_s[:, G, 512 * h : 512 * (h + 1)], start=(G == 0), stop=(G == NGO - 1))
 
         def ye(g, j):
-            yt[(g, j)] = work.tile([P, IN], F32, name="y", tag="y", bufs=5)
+            yt[(g, j)] = work.tile([P, IN], F32, name="y", tag="y", bufs=4)
             for h in range(NH):
                 nc.scalar.activation(out=yt[(g, j)][:, 512 * h : 512 * (h + 1)], in_=accp[(g, j, h)][:], func=ACT.Copy, scale=lam[:, g, j : j + 1])
 
         def pep(g, j):
-            nc.vector.scalar_tensor_tensor(out=junk_v[:], in0=yt[(g, j)][:], scalar=1.0, in1=xt[(g, j)][:], op0=ALU.mult, op1=ALU.mult, accum_out=st[("dpy", g)][:, j : j + 1])
+            nc.vector.scalar_tensor_tensor(out=junk_v[:], in0=yt[(g, j)][:], scalar=1.0, in1=xt[(g, j)][:], op0=ALU.mult, op1=ALU.mult, accum_out=st_[("dpy", g)][:, j : j + 1])
 
         def co(g, j):
-            nc.vector.scalar_tensor_tensor(out=st[("coef", g)][:, j : j + 1], in0=st[("dpy", g)][:, j : j + 1], scalar=st[("alpha", g)][:, j : j + 1], in1=st[("bg", g)][:, j : j + 1], op0=ALU.mult, op1=ALU.subtract)
+            nc.vector.scalar_tensor_tensor(out=st_[("coef", g)][:, j : j + 1], in0=st_[("dpy", g)][:, j : j + 1], scalar=st_[("alpha", g)][:, j : j + 1], in1=st_[("bg", g)][:, j : j + 1], op0=ALU.mult, op1=ALU.subtract)
 
         def fi(g, j):
-            nc.vector.scalar_tensor_tensor(out=yt[(g, j)][:], in0=xt[(g, j)][:], scalar=st[("coef", g)][:, j : j + 1], in1=yt[(g, j)][:], op0=ALU.mult, op1=ALU.add)
+            nc.vector.scalar_tensor_tensor(out=yt[(g, j)][:], in0=xt[(g, j)][:], scalar=st_[("coef", g)][:, j : j + 1], in1=yt[(g, j)][:], op0=ALU.mult, op1=ALU.add)
             nc.sync.dma_start(out=o0v[:, g, j, :], in_=yt[(g, j)][:])
 
         def it(g):
@@ -213,22 +224,22 @@ def tile_lorentz_fully_connected_mlr_angle_v_kernel(tc, x, z, a, xn, q, grad_out
             nc.vector.quantize_mx(out=ps_c[:, g, :].bitcast(E4), scales=ps_s[:, g, :], in_=grp[("p", g)][:].rearrange("p w j -> p (w j)"))
 
         def xx(g, j):
-            nc.scalar.activation(out=junk_a[:], in_=xt[(g, j)][:], func=ACT.Square, accum_out=st[("nx2", g)][:, j : j + 1])
+            nc.scalar.activation(out=junk_a[:], in_=xt[(g, j)][:], func=ACT.Square, accum_out=st_[("nx2", g)][:, j : j + 1])
 
         def xx_v(g, j):
-            nc.vector.scalar_tensor_tensor(out=junk_v[:], in0=xt[(g, j)][:], scalar=1.0, in1=xt[(g, j)][:], op0=ALU.mult, op1=ALU.mult, accum_out=st[("nx2", g)][:, j : j + 1])
+            nc.vector.scalar_tensor_tensor(out=junk_v[:], in0=xt[(g, j)][:], scalar=1.0, in1=xt[(g, j)][:], op0=ALU.mult, op1=ALU.mult, accum_out=st_[("nx2", g)][:, j : j + 1])
 
         def nxs(g):
-            nc.scalar.activation(out=st[("nx", g)][:], in_=st[("nx2", g)][:], func=ACT.Sqrt)
+            nc.scalar.activation(out=st_[("nx", g)][:], in_=st_[("nx2", g)][:], func=ACT.Sqrt)
 
         def inx(g):
-            nc.vector.reciprocal(out=st[("inx", g)][:], in_=st[("nx", g)][:])
-            nc.vector.tensor_tensor(out=st[("beta", g)][:], in0=sh[:, g, :], in1=st[("inx", g)][:], op=ALU.mult)
-            nc.vector.tensor_tensor(out=st[("inx2", g)][:], in0=st[("inx", g)][:], in1=st[("inx", g)][:], op=ALU.mult)
-            nc.vector.tensor_tensor(out=st[("alpha", g)][:], in0=t0[:, g, :], in1=st[("inx2", g)][:], op=ALU.mult)
+            nc.vector.reciprocal(out=st_[("inx", g)][:], in_=st_[("nx", g)][:])
+            nc.vector.tensor_tensor(out=st_[("beta", g)][:], in0=sh[:, g, :], in1=st_[("inx", g)][:], op=ALU.mult)
+            nc.vector.tensor_tensor(out=st_[("inx2", g)][:], in0=st_[("inx", g)][:], in1=st_[("inx", g)][:], op=ALU.mult)
+            nc.vector.tensor_tensor(out=st_[("alpha", g)][:], in0=t0[:, g, :], in1=st_[("inx2", g)][:], op=ALU.mult)
 
         def bg(g):
-            nc.vector.tensor_tensor(out=st[("bg", g)][:], in0=st[("beta", g)][:], in1=st[("gsum", g)][:], op=ALU.mult)
+            nc.vector.tensor_tensor(out=st_[("bg", g)][:], in0=st_[("beta", g)][:], in1=st_[("gsum", g)][:], op=ALU.mult)
 
         def qf(g, b0, b1):
             for b in range(b0, b1):
@@ -238,15 +249,6 @@ def tile_lorentz_fully_connected_mlr_angle_v_kernel(tc, x, z, a, xn, q, grad_out
                     trp[("s", g, 2)] = psum.tile([P, 2 * QN], F32, name="th", tag="th", bufs=1)
                 for j in range(NJ):
                     nc.tensor.matmul(out=trp[("s", g, b // 3)][:, QN * (b % 3) : QN * (b % 3 + 1)], lhsT=x1[(g, j)][:, P * b : P * (b + 1)], rhs=qt[(g, j)][:, b, 0:QN], start=(j == 0), stop=(j == NJ - 1))
-
-        def hf(g):
-            for k in range(2):
-                ht = psum.tile([P, 4, P], F32, name="tr", tag="tr", bufs=2)
-                for b in range(4):
-                    for j in range(NJ):
-                        nc.tensor.matmul(out=ht[:, b, :], lhsT=x2[(g, j)][:, P * (4 * k + b) : P * (4 * k + b + 1)], rhs=ident_f[:], is_transpose=True, start=(j == 0), stop=(j == NJ - 1))
-                for b in range(4):
-                    nc.scalar.activation(out=junk_a[:, 0:P], in_=ht[:, b, :], func=ACT.Copy, accum_out=hpart[:, g, 4 * k + b : 4 * k + b + 1])
 
         def qse(g):
             for k in range(2):
@@ -272,11 +274,13 @@ def tile_lorentz_fully_connected_mlr_angle_v_kernel(tc, x, z, a, xn, q, grad_out
         nc.vector.memset(qs_acc[:], 0.0)
         nc.sync.dma_start(out=xn_t[:], in_=xnv)
         nc.sync.dma_start(out=a_rows[0:NB, :], in_=a.rearrange("(b m) -> b m", m=P))
+        load_q(0, 0)
+        load_q(0, 1)
         for k in range(2):
             nat[("r", k)] = work.tile([P, 4, IN], BF16, name="nat", tag="nat", bufs=2)
             nc.sync.dma_start(out=nat[("r", k)][:], in_=znv[:, 4 * k : 4 * (k + 1), :])
-        for j in range(NJ):
-            load_q(0, j)
+        load_q(0, 2)
+        load_q(0, 3)
         for G in range(NGO):
             nat[("z", G)] = work.tile([P, NJ, IN], BF16, name="natz", tag="natz", bufs=2)
             nc.sync.dma_start(out=nat[("z", G)][:], in_=zkv[:, G, :, :])
@@ -284,7 +288,6 @@ def tile_lorentz_fully_connected_mlr_angle_v_kernel(tc, x, z, a, xn, q, grad_out
             load_g(0, j)
         for j in range(NJ):
             load_x(0, j)
-        zt = {}
 
         nc.scalar.activation(out=ep[:], in_=xn_t[:], func=ACT.Exp, scale=1.0 / SK)
         nc.scalar.activation(out=em[:], in_=xn_t[:], func=ACT.Exp, scale=-1.0 / SK)
@@ -300,8 +303,8 @@ def tile_lorentz_fully_connected_mlr_angle_v_kernel(tc, x, z, a, xn, q, grad_out
             sq(0, j)
             ab(0, j)
             sr(0, j)
-            if j == 1:
-                nc.scalar.activation(out=zn_mb[:], in_=zn2[:], func=ACT.Sqrt)
+            sgn(0, j)
+        nc.scalar.activation(out=zn_mb[:], in_=zn2[:], func=ACT.Sqrt)
         nc.vector.tensor_tensor(out=ch[:], in0=ep[:], in1=em[:], op=ALU.add)
         nc.vector.tensor_tensor(out=sh[:], in0=ep[:], in1=em[:], op=ALU.subtract)
         nc.vector.tensor_scalar(out=chn[:], in0=ch[:].unsqueeze(3).to_broadcast([P, NG, NJ, 2]), scalar1=-0.5 * SK, scalar2=None, op0=ALU.mult)
@@ -311,7 +314,7 @@ def tile_lorentz_fully_connected_mlr_angle_v_kernel(tc, x, z, a, xn, q, grad_out
         nc.vector.tensor_tensor(out=sa_mb[:], in0=ea[:], in1=eb[:], op=ALU.subtract)
         nc.vector.tensor_scalar(out=ca_mb[:], in0=ca_mb[:], scalar1=0.5, scalar2=None, op0=ALU.mult)
         nc.vector.tensor_scalar(out=sa_mb[:], in0=sa_mb[:], scalar1=0.5, scalar2=None, op0=ALU.mult)
-        bcast(ca_mb, "ca", "acc", 3)
+        bcast(ca_mb, "ca", "acc", 2)
         nc.vector.reciprocal(out=rxn[:], in_=xn_t[:])
         nc.vector.tensor_scalar(out=sh[:], in0=sh[:], scalar1=0.5, scalar2=None, op0=ALU.mult)
         nc.vector.tensor_scalar(out=ch[:], in0=ch[:], scalar1=0.5, scalar2=None, op0=ALU.mult)
@@ -337,19 +340,21 @@ def tile_lorentz_fully_connected_mlr_angle_v_kernel(tc, x, z, a, xn, q, grad_out
                 fi(g, j)
 
         def m_out(b):
-            o1 = work.tile([P, IN], F32, name="y", tag="y", bufs=5)
+            o1 = work.tile([P, IN], F32, name="y", tag="y", bufs=4)
             for h in range(NH):
                 tag, bufs = M_BANKS[(NH * b + h) % len(M_BANKS)]
                 macc = psum.tile([P, 512], F32, name=tag, tag=tag, bufs=bufs)
                 for g in range(NG):
                     nc.tensor.matmul_mx(out=macc[:], lhsT=ddt_c[:, g, P * b : P * (b + 1)].bitcast(E5), lhsT_scale=ddt_s[:, g, P * b : P * (b + 1)],
                                         rhs=ps_c[:, g, 512 * h : 512 * (h + 1)].bitcast(E4), rhs_scale=ps_s[:, g, 512 * h : 512 * (h + 1)], start=(g == 0), stop=(g == NG - 1))
-                nc.vector.scalar_tensor_tensor(out=o1[:, 512 * h : 512 * (h + 1)], in0=zt[b][:, 512 * h : 512 * (h + 1)], scalar=so[:, b : b + 1], in1=macc[:], op0=ALU.mult, op1=ALU.add)
+                nc.vector.scalar_tensor_tensor(out=o1[:, 512 * h : 512 * (h + 1)], in0=nat[("e", b // 4)][:, b % 4, 512 * h : 512 * (h + 1)], scalar=so[:, b : b + 1], in1=macc[:], op0=ALU.mult, op1=ALU.add)
             nc.sync.dma_start(out=o1v[:, b, :], in_=o1[:])
 
-        def load_z(b):
-            zt[b] = work.tile([P, IN], BF16, name="x", tag="x", bufs=8)
-            nc.sync.dma_start(out=zt[b][:], in_=znv[:, b, :])
+        def load_z(k):
+            nat[("e", k)] = work.tile([P, 4, IN], BF16, name="nat", tag="nat", bufs=2)
+            nc.sync.dma_start(out=nat[("e", k)][:], in_=znv[:, 4 * k : 4 * (k + 1), :])
+
+        bcast_out("ca", ca_bc)
 
         for g in range(NG):
             more = g + 1 < NG
@@ -357,6 +362,11 @@ def tile_lorentz_fully_connected_mlr_angle_v_kernel(tc, x, z, a, xn, q, grad_out
                 for j in range(NJ):
                     sr(g, j)
                 nxs(g)
+            for b in range(4):
+                st(g, b)
+            for j in range(NJ):
+                ar(g, j)
+            if g > 0:
                 qse(g - 1)
                 epi(g - 1, (2, 3))
                 if more:
@@ -365,60 +375,60 @@ def tile_lorentz_fully_connected_mlr_angle_v_kernel(tc, x, z, a, xn, q, grad_out
                     load_q(g + 1, 0)
                     put_ch(g + 1, 0)
                     load_g(g + 1, 0)
-                else:
-                    for b in range(4):
-                        load_z(b)
-            s_add(g, 0)
-            if g == 0:
+                the(g - 1)
+                inx(g)
+            else:
                 z_codes(0)
-            s_add(g, 1)
-            if g == 0:
                 nc.vector.reciprocal(out=izn[:], in_=zn_mb[:])
                 nc.vector.tensor_tensor(out=c_mb[:], in0=sa_mb[:], in1=zn_mb[:], op=ALU.mult)
-                bcast(c_mb, "c", "tr", 2)
+                bcast(c_mb, "c", "qs", 2)
                 z_quant(0)
-            s_add(g, 2)
-            if g == 0:
                 z_codes(1)
                 for j in range(NJ):
                     load_x(1, j)
                 load_q(1, 0)
                 put_ch(1, 0)
                 load_g(1, 0)
-            s_add(g, 3)
-            if g == 0:
+                bcast_out("c", c_bc)
                 z_quant(1)
             for j in range(NJ):
-                ar(g, j)
-            if g > 0:
-                the(g - 1)
-                inx(g)
-            else:
-                bcast_out("ca", ca_bc)
-                bcast_out("c", c_bc)
+                gg(g, j)
+            g_t(g, 0)
             for j in range(NJ):
                 ps(g, j)
-            for j in range(NJ):
-                ln(g, j)
-            for j in range(NJ):
-                sgn(g, j)
+            for b in range(4):
+                ln_t(g, b)
+                st(g, b + 4)
             for j in range(NJ):
                 b_mul(g, j)
             qf(g, 0, 3)
+            hs_(g, 0)
+            ln_t(g, 4)
             dd_mul(g, 0)
             tr(g, 0)
+            hs_(g, 1)
+            ln_t(g, 5)
+            g_t(g, 1)
             dd_mul(g, 1)
             tr(g, 1)
             dd_mul(g, 2)
+            hs_(g, 2)
+            ln_t(g, 6)
             dd_mul(g, 3)
+            hs_(g, 3)
+            ln_t(g, 7)
+            g_t(g, 2)
             te(g, 0)
             tr(g, 2)
             te(g, 1)
             tr(g, 3)
             qf(g, 3, 8)
             ip(g)
+            hs_(g, 4)
             te(g, 2)
             qo(g, 0)
+            hs_(g, 5)
+            g_t(g, 3)
             te(g, 3)
             if g == 0:
                 for j in range(NJ):
@@ -429,8 +439,10 @@ def tile_lorentz_fully_connected_mlr_angle_v_kernel(tc, x, z, a, xn, q, grad_out
             qo(g, 1)
             gs_sum(g, 1)
             it(g)
+            hs_(g, 6)
             qo(g, 2)
             gs_sum(g, 2)
+            hs_(g, 7)
             qt_(g)
             qo(g, 3)
             gs_sum(g, 3)
@@ -440,26 +452,22 @@ def tile_lorentz_fully_connected_mlr_angle_v_kernel(tc, x, z, a, xn, q, grad_out
             if more:
                 for j in range(NJ):
                     xx(g + 1, j)
-            for j in range(NJ):
-                mx(g, j)
-                ye(g, j)
-            for j in range(NJ):
-                gg(g, j)
+            if more:
+                for j in range(NJ):
+                    mx(g, j)
+                    ye(g, j)
             if more:
                 for j in range(1, NJ):
                     load_q(g + 1, j)
                     put_ch(g + 1, j)
-            for j in range(NJ):
-                ha(g, j)
-            if more:
                 for j in range(1, NJ):
                     load_g(g + 1, j)
-            if more:
                 for j in range(NJ):
                     sq(g + 1, j)
                 for j in range(NJ):
                     ab(g + 1, j)
-                hf(g)
+                for j in range(NJ):
+                    sgn(g + 1, j)
                 epi(g, (0, 1))
 
         g = NG - 1
@@ -469,27 +477,20 @@ def tile_lorentz_fully_connected_mlr_angle_v_kernel(tc, x, z, a, xn, q, grad_out
         gz = keep.tile([P, NB], F32, name="gz")
         so = keep.tile([P, NB], F32, name="so")
         sums = qs_acc[:, 0 : NB * QN].rearrange("p (b n) -> p b n", n=QN)
-        hf(g)
+        load_z(0)
+        load_z(1)
         qse(g)
-        for j in range(NJ):
-            pep(g, j)
         the(g)
-        for j in range(NJ):
-            co(g, j)
         nc.vector.tensor_tensor(out=dg[:], in0=sums[:, :, 0:P], in1=ident_f[:].unsqueeze(1).to_broadcast([P, NB, P]), op=ALU.mult)
         nc.vector.tensor_reduce(out=hs[:], in_=hpart[:].rearrange("p g b -> p b g"), axis=AX.X, op=ALU.add)
         nc.vector.tensor_tensor(out=gz[:], in0=sa_mb[:], in1=sums[:, :, P], op=ALU.mult)
         nc.vector.tensor_reduce(out=s1b[:], in_=dg[:], axis=AX.X, op=ALU.add)
         nc.vector.scalar_tensor_tensor(out=gz[:], in0=hs[:], scalar=1.0 / SK, in1=gz[:], op0=ALU.mult, op1=ALU.add)
-        fi(g, 0)
         nc.vector.scalar_tensor_tensor(out=gz[:], in0=s1b[:], scalar=-1.0 / SK, in1=gz[:], op0=ALU.mult, op1=ALU.add)
-        fi(g, 1)
         nc.vector.tensor_tensor(out=so[:], in0=gz[:], in1=izn[:], op=ALU.mult)
-        load_z(4)
-        load_z(5)
-        fi(g, 2)
-        fi(g, 3)
-        load_z(6)
-        load_z(7)
-        for b in range(NB):
-            m_out(b)
+        for j in range(NJ):
+            mx(g, j)
+            ye(g, j)
+            m_out(2 * j)
+            epi(g, (j,))
+            m_out(2 * j + 1)

@@ -89,6 +89,9 @@ def tile_lorentz_fully_connected_mlr_angle_v_kernel(tc, x, z, a, xn, q, grad_out
             for nm in ("nx2", "nx", "inx", "inx2", "alpha", "beta", "gsum", "bg", "dpy", "coef"):
                 st_[(nm, g)] = keep.tile([P, NJ], F32, name="%s%d" % (nm, g))
 
+        def interleave(dst, src):
+            nc.vector.tensor_copy(out=dst[:].rearrange("p (c i) j -> p c j i", i=4), in_=src[:].rearrange("p j (c i) -> p c j i", i=4))
+
         def load_q(g, j):
             qt[(g, j)] = work.tile([P, NB, QW], F32, name="q", tag="q", bufs=5)
             nc.sync.dma_start(out=qt[(g, j)][:, :, 0:P], in_=qv[:, g, j, :].rearrange("p (b n) -> p b n", n=P))
@@ -129,7 +132,7 @@ def tile_lorentz_fully_connected_mlr_angle_v_kernel(tc, x, z, a, xn, q, grad_out
 
         def sgn(g, j):
             sg[(g, j)] = work.tile([P, OUT], BF16, name="sg", tag="sg", bufs=4)
-            nc.scalar.activation(out=blocks(sg[(g, j)]), in_=qt[(g, j)][:, :, 0:P], func=ACT.Sign)
+            nc.vector.tensor_scalar(out=blocks(sg[(g, j)]), in0=qt[(g, j)][:, :, 0:P], scalar1=0.0, scalar2=0.5, op0=ALU.is_ge, op1=ALU.subtract)
 
         def b_mul(g, j):
             nc.vector.tensor_tensor(out=x1[(g, j)][:], in0=gt[(g, j)][:], in1=x1[(g, j)][:], op=ALU.mult)
@@ -206,7 +209,7 @@ def tile_lorentz_fully_connected_mlr_angle_v_kernel(tc, x, z, a, xn, q, grad_out
 
         def it(g):
             grp[("d", g)] = work.tile([P, OUT, NJ], BF16, name="grp", tag="grp", bufs=1, align_bytes=64)
-            nc.vector.tensor_copy(out=grp[("d", g)][:], in_=nat[("d", g)][:].rearrange("p j w -> p w j"))
+            interleave(grp[("d", g)], nat[("d", g)])
 
         def qt_(g):
             nc.vector.quantize_mx(out=ddt_c[:, g, :].bitcast(E5), scales=ddt_s[:, g, :], in_=grp[("d", g)][:].rearrange("p w j -> p (w j)"))
@@ -218,7 +221,7 @@ def tile_lorentz_fully_connected_mlr_angle_v_kernel(tc, x, z, a, xn, q, grad_out
 
         def ip(g):
             grp[("p", g)] = work.tile([P, IN, NJ], BF16, name="grp", tag="grp", bufs=1, align_bytes=64)
-            nc.vector.tensor_copy(out=grp[("p", g)][:], in_=nat[("p", g)][:].rearrange("p j w -> p w j"))
+            interleave(grp[("p", g)], nat[("p", g)])
 
         def qp(g):
             nc.vector.quantize_mx(out=ps_c[:, g, :].bitcast(E4), scales=ps_s[:, g, :], in_=grp[("p", g)][:].rearrange("p w j -> p (w j)"))
@@ -326,7 +329,7 @@ def tile_lorentz_fully_connected_mlr_angle_v_kernel(tc, x, z, a, xn, q, grad_out
 
         def z_codes(G):
             grp[("z", G)] = work.tile([P, IN, NJ], BF16, name="grp", tag="grp", bufs=1, align_bytes=64)
-            nc.vector.tensor_copy(out=grp[("z", G)][:], in_=nat[("z", G)][:].rearrange("p j w -> p w j"))
+            interleave(grp[("z", G)], nat[("z", G)])
 
         def z_quant(G):
             nc.vector.quantize_mx(out=z_c[:, G, :].bitcast(E4), scales=z_s[:, G, :], in_=grp[("z", G)][:].rearrange("p w j -> p (w j)"))
@@ -485,7 +488,7 @@ def tile_lorentz_fully_connected_mlr_angle_v_kernel(tc, x, z, a, xn, q, grad_out
         nc.vector.tensor_reduce(out=hs[:], in_=hpart[:].rearrange("p g b -> p b g"), axis=AX.X, op=ALU.add)
         nc.vector.tensor_tensor(out=gz[:], in0=sa_mb[:], in1=sums[:, :, P], op=ALU.mult)
         nc.vector.tensor_reduce(out=s1b[:], in_=dg[:], axis=AX.X, op=ALU.add)
-        nc.vector.scalar_tensor_tensor(out=gz[:], in0=hs[:], scalar=1.0 / SK, in1=gz[:], op0=ALU.mult, op1=ALU.add)
+        nc.vector.scalar_tensor_tensor(out=gz[:], in0=hs[:], scalar=2.0 / SK, in1=gz[:], op0=ALU.mult, op1=ALU.add)
         nc.vector.scalar_tensor_tensor(out=gz[:], in0=s1b[:], scalar=-1.0 / SK, in1=gz[:], op0=ALU.mult, op1=ALU.add)
         nc.vector.tensor_tensor(out=so[:], in0=gz[:], in1=izn[:], op=ALU.mult)
         for j in range(NJ):

import math
from contextlib import ExitStack

import concourse.mybir as mybir
from concourse.masks import make_identity

F32 = mybir.dt.float32
BF16 = mybir.dt.bfloat16
U32 = mybir.dt.uint32
U8 = mybir.dt.uint8
I32 = mybir.dt.int32
E4 = mybir.dt.float8_e4m3fn_x4
E5 = mybir.dt.float8_e5m2_x4
ALU = mybir.AluOpType
ACT = mybir.ActivationFunctionType
AX = mybir.AxisListType

P = 128
NG = 4
NJ = 4
OUT = 1024
IN = 1024
NB = OUT // P
NGO = OUT // 512
NH = IN // 512
QW = 136
QN = 130
SK = math.sqrt(0.1)
FLOPS = 2 * 2 * 2048 * 1024 * 1024
M_BANKS = (("tr", 2), ("tr", 2), ("qs", 2), ("qs", 2), ("gt", 1))


def tile_lorentz_fully_connected_mlr_angle_v_kernel(tc, x, z, a, xn, q, grad_out, out_0, out_1):
    nc = tc.nc
    xv = x.rearrange("g (p j) i -> p g j i", j=NJ)
    qv = q.rearrange("g (p j) o -> p g j o", j=NJ)
    gv = grad_out.rearrange("g (p j) o -> p g j o", j=NJ)
    o0v = out_0.rearrange("g (p j) i -> p g j i", j=NJ)
    xnv = xn.rearrange("g (p j) one -> p g (j one)", j=NJ)
    zkv = z.rearrange("(G p j) i -> p G j i", G=NGO, j=NJ)
    znv = z.rearrange("(b m) i -> m b i", m=P)
    o1v = out_1.rearrange("(b m) i -> m b i", m=P)

    with ExitStack() as ctx:
        keep = ctx.enter_context(tc.tile_pool(name="keep", bufs=1))
        work = ctx.enter_context(tc.tile_pool(name="work", bufs=2))
        psum = ctx.enter_context(tc.psum_pool(name="psum", bufs=1))

        ident_f = keep.tile([P, P], F32, name="ident_f")
        ident_b = keep.tile([P, P], BF16, name="ident_b")
        ddt_c = keep.tile([P, NG, OUT], U32, name="ddt_c", align_bytes=64)
        ddt_s = keep.tile([P, NG, OUT], U8, name="ddt_s", align_bytes=64)
        ps_c = keep.tile([P, NG, IN], U32, name="ps_c", align_bytes=64)
        ps_s = keep.tile([P, NG, IN], U8, name="ps_s", align_bytes=64)
        z_c = keep.tile([P, NGO, IN], U32, name="z_c", align_bytes=64)
        z_s = keep.tile([P, NGO, IN], U8, name="z_s", align_bytes=64)
        ca_bc = keep.tile([P, OUT], F32, name="ca_bc")
        c_bc = keep.tile([P, OUT], F32, name="c_bc")
        qs_acc = keep.tile([P, NB * QN], F32, name="qs_acc")
        hpart = keep.tile([P, NG, NB], F32, name="hpart")
        junk_v = keep.tile([P, OUT], F32, name="junk_v")
        junk_a = keep.tile([P, IN], BF16, name="junk_a")
        one = keep.tile([P, 1], F32, name="one")
        a_rows = keep.tile([P, P], BF16, name="a_rows")
        a_mb = keep.tile([P, NB], F32, name="a_mb")
        ea = keep.tile([P, NB], F32, name="ea")
        eb = keep.tile([P, NB], F32, name="eb")
        ca_mb = keep.tile([P, NB], F32, name="ca_mb")
        sa_mb = keep.tile([P, NB], F32, name="sa_mb")
        zn2 = keep.tile([P, NB], F32, name="zn2")
        zn_mb = keep.tile([P, NB], F32, name="zn_mb")
        izn = keep.tile([P, NB], F32, name="izn")
        c_mb = keep.tile([P, NB], F32, name="c_mb")
        xn_t = keep.tile([P, NG, NJ], F32, name="xn_t")
        ep = keep.tile([P, NG, NJ], F32, name="ep")
        em = keep.tile([P, NG, NJ], F32, name="em")
        sh = keep.tile([P, NG, NJ], F32, name="sh")
        ch = keep.tile([P, NG, NJ], F32, name="ch")
        rxn = keep.tile([P, NG, NJ], F32, name="rxn")
        lam = keep.tile([P, NG, NJ], F32, name="lam")
        ilam = keep.tile([P, NG, NJ], F32, name="ilam")
        t0 = keep.tile([P, NG, NJ], F32, name="t0")
        chn = keep.tile([P, NG, NJ, 2], F32, name="chn")

        qt, gt, xt, x1, x2, aq, sg, nat, grp = {}, {}, {}, {}, {}, {}, {}, {}, {}
        trp, go, oc, osc, accp, yt, st_, lt = {}, {}, {}, {}, {}, {}, {}, {}

        for g in range(NG):
            for nm in ("nx2", "nx", "inx", "inx2", "alpha", "beta", "gsum", "bg", "dpy", "coef"):
                st_[(nm, g)] = keep.tile([P, NJ], F32, name="%s%d" % (nm, g))

        def interleave(dst, src):
            nc.vector.tensor_copy(out=dst[:].rearrange("p (c i) j -> p c j i", i=4), in_=src[:].rearrange("p j (c i) -> p c j i", i=4))

        def load_q(g, j):
            qt[(g, j)] = work.tile([P, NB, QW], F32, name="q", tag="q", bufs=5)
            nc.sync.dma_start(out=qt[(g, j)][:, :, 0:P], in_=qv[:, g, j, :].rearrange("p (b n) -> p b n", n=P))

        def put_ch(g, j):
            nc.gpsimd.tensor_copy(out=qt[(g, j)][:, :, P:QN], in_=chn[:, g, j, :].unsqueeze(1).to_broadcast([P, NB, 2]))

        def blocks(t):
            return t[:].rearrange("p (b n) -> p b n", n=P)

        def load_g(g, j):
            gt[(g, j)] = work.tile([P, OUT], BF16, name="g", tag="g", bufs=5)
            nc.sync.dma_start(out=gt[(g, j)][:], in_=gv[:, g, j, :])

        def load_x(g, j):
            xt[(g, j)] = work.tile([P, IN], BF16, name="x", tag="x", bufs=8)
            nc.sync.dma_start(out=xt[(g, j)][:], in_=xv[:, g, j, :])

        def sq(g, j):
            x1[(g, j)] = work.tile([P, OUT], F32, name="x1", tag="x1", bufs=4)
            nc.scalar.activation(out=blocks(x1[(g, j)]), in_=qt[(g, j)][:, :, 0:P], func=ACT.Square)

        def sr(g, j):
            x2[(g, j)] = work.tile([P, OUT], F32, name="x2", tag="x2", bufs=4)
            nc.scalar.activation(out=x2[(g, j)][:], in_=x1[(g, j)][:], func=ACT.Sqrt, bias=one[:], scale=1.0)

        def ar(g, j):
            nc.scalar.activation(out=x1[(g, j)][:], in_=x1[(g, j)][:], func=ACT.Abs_reciprocal_sqrt, bias=one[:], scale=1.0)

        def ab(g, j):
            if g == 0:
                aq[(g, j)] = work.tile([P, OUT], F32, name="y", tag="y", bufs=4)[:]
            else:
                if j % 2 == 0:
                    aq[("pair", g, j // 2)] = work.tile([P, 2, OUT], F32, name="natz", tag="natz", bufs=2)
                aq[(g, j)] = aq[("pair", g, j // 2)][:, j % 2, :]
            nc.scalar.activation(out=aq[(g, j)].rearrange("p (b n) -> p b n", n=P), in_=qt[(g, j)][:, :, 0:P], func=ACT.Abs)

        def sgn(g, j):
            sg[(g, j)] = work.tile([P, OUT], BF16, name="sg", tag="sg", bufs=4)
            nc.vector.tensor_scalar(out=blocks(sg[(g, j)]), in0=qt[(g, j)][:, :, 0:P], scalar1=0.0, scalar2=0.5, op0=ALU.is_ge, op1=ALU.subtract)

        def b_mul(g, j):
            nc.vector.tensor_tensor(out=x1[(g, j)][:], in0=gt[(g, j)][:], in1=x1[(g, j)][:], op=ALU.mult)

        def dd_mul(g, j):
            if j == 0:
                nat[("d", g)] = work.tile([P, NJ, OUT], BF16, name="nat", tag="nat", bufs=2)
            nc.vector.tensor_tensor(out=nat[("d", g)][:, j, :], in0=x1[(g, j)][:], in1=ca_bc[:], op=ALU.mult)

        def gs_sum(g, j):
            nc.vector.scalar_tensor_tensor(out=junk_v[:], in0=x1[(g, j)][:], scalar=1.0, in1=c_bc[:], op0=ALU.mult, op1=ALU.mult, accum_out=st_[("gsum", g)][:, j : j + 1])

        def gg(g, j):
            nc.vector.tensor_tensor(out=sg[(g, j)][:], in0=gt[(g, j)][:], in1=sg[(g, j)][:], op=ALU.mult)

        def st(g, b):
            tag = ("tr", "tr", "acc", "acc")[b % 4]
            trp[("st", g, b)] = psum.tile([P, NJ, P], F32, name=tag, tag=tag, bufs=2)
            cols = slice(P * b, P * (b + 1))
            for j in range(NJ):
                nc.tensor.matmul(out=trp[("st", g, b)][:, j, :], lhsT=aq[(g, j)][:, cols], rhs=ident_f[:], is_transpose=True, start=True, stop=False)
                nc.tensor.matmul(out=trp[("st", g, b)][:, j, :], lhsT=x2[(g, j)][:, cols], rhs=ident_f[:], is_transpose=True, start=False, stop=True)

        def ln_t(g, b):
            lt[(g, b)] = work.tile([P, NJ * P], F32, name="lt", tag="lt", bufs=4)
            nc.scalar.activation(out=lt[(g, b)][:], in_=trp[("st", g, b)][:].rearrange("p j t -> p (j t)"), func=ACT.Ln)

        def g_t(g, k):
            trp[("gt", g, k)] = psum.tile([P, 2, NJ, P], BF16, name="gt", tag="gt", bufs=1)
            for b in (2 * k, 2 * k + 1):
                for j in range(NJ):
                    nc.tensor.transpose(out=trp[("gt", g, k)][:, b % 2, j, :], in_=sg[(g, j)][:, P * b : P * (b + 1)], identity=ident_b[:])

        def hs_(g, b):
            nc.vector.scalar_tensor_tensor(out=junk_v[:, 0 : NJ * P], in0=trp[("gt", g, b // 2)][:, b % 2, :, :].rearrange("p j t -> p (j t)"), scalar=1.0, in1=lt[(g, b)][:], op0=ALU.mult, op1=ALU.mult, accum_out=hpart[:, g, b : b + 1])

        def tr(g, j):
            trp[(g, j)] = psum.tile([P, NGO, 2, P], F32, name="tr", tag="tr", bufs=2)
            words = nat[("d", g)][:, j, :].bitcast(F32)
            for G in range(NGO):
                for u in range(2):
                    nc.tensor.transpose(out=trp[(g, j)][:, G, u, :], in_=words[:, 256 * G + u : 256 * (G + 1) : 2], identity=ident_f[:])

        def te(g, j):
            go[(g, j)] = work.tile([P, NGO * P * 4], BF16, name="go", tag="go", bufs=3, align_bytes=64)
            nc.scalar.copy(out=go[(g, j)][:].bitcast(F32).rearrange("p (G r u) -> p G r u", G=NGO, u=2), in_=trp[(g, j)][:].rearrange("p G u r -> p G r u"))

        def qo(g, j):
            oc[(g, j)] = work.tile([P, NGO * P], U32, name="oc", tag="oc", bufs=5, align_bytes=64)
            osc[(g, j)] = work.tile([P, NGO * P], U8, name="osc", tag="osc", bufs=5, align_bytes=64)
            nc.vector.quantize_mx(out=oc[(g, j)][:].bitcast(E5), scales=osc[(g, j)][:], in_=go[(g, j)][:])

        def mx(g, j):
            for h in range(NH):
                accp[(g, j, h)] = psum.tile([P, 512], F32, name="acc", tag="acc", bufs=2)
                for G in range(NGO):
                    nc.tensor.matmul_mx(out=accp[(g, j, h)][:], lhsT=oc[(g, j)][:, P * G : P * (G + 1)].bitcast(E5), lhsT_scale=osc[(g, j)][:, P * G : P * (G + 1)],
                                        rhs=z_c[:, G, 512 * h : 512 * (h + 1)].bitcast(E4), rhs_scale=z_s[:, G, 512 * h : 512 * (h + 1)], start=(G == 0), stop=(G == NGO - 1))

        def ye(g, j):
            yt[(g, j)] = work.tile([P, IN], F32, name="y", tag="y", bufs=4)
            for h in range(NH):
                nc.scalar.activation(out=yt[(g, j)][:, 512 * h : 512 * (h + 1)], in_=accp[(g, j, h)][:], func=ACT.Copy, scale=lam[:, g, j : j + 1])

        def pep(g, j):
            nc.vector.scalar_tensor_tensor(out=junk_v[:], in0=yt[(g, j)][:], scalar=1.0, in1=xt[(g, j)][:], op0=ALU.mult, op1=ALU.mult, accum_out=st_[("dpy", g)][:, j : j + 1])

        def co(g, j):
            nc.vector.scalar_tensor_tensor(out=st_[("coef", g)][:, j : j + 1], in0=st_[("dpy", g)][:, j : j + 1], scalar=st_[("alpha", g)][:, j : j + 1], in1=st_[("bg", g)][:, j : j + 1], op0=ALU.mult, op1=ALU.subtract)

        def fi(g, j):
            nc.vector.scalar_tensor_tensor(out=yt[(g, j)][:], in0=xt[(g, j)][:], scalar=st_[("coef", g)][:, j : j + 1], in1=yt[(g, j)][:], op0=ALU.mult, op1=ALU.add)
            nc.sync.dma_start(out=o0v[:, g, j, :], in_=yt[(g, j)][:])

        def it(g):
            grp[("d", g)] = work.tile([P, OUT, NJ], BF16, name="grp", tag="grp", bufs=1, align_bytes=64)
            interleave(grp[("d", g)], nat[("d", g)])

        def qt_(g):
            nc.vector.quantize_mx(out=ddt_c[:, g, :].bitcast(E5), scales=ddt_s[:, g, :], in_=grp[("d", g)][:].rearrange("p w j -> p (w j)"))

        def ps(g, j):
            if j == 0:
                nat[("p", g)] = work.tile([P, NJ, IN], BF16, name="nat", tag="nat", bufs=2)
            nc.vector.tensor_scalar(out=nat[("p", g)][:, j, :], in0=xt[(g, j)][:], scalar1=lam[:, g, j : j + 1], scalar2=None, op0=ALU.mult)

        def ip(g):
            grp[("p", g)] = work.tile([P, IN, NJ], BF16, name="grp", tag="grp", bufs=1, align_bytes=64)
            interleave(grp[("p", g)], nat[("p", g)])

        def qp(g):
            nc.vector.quantize_mx(out=ps_c[:, g, :].bitcast(E4), scales=ps_s[:, g, :], in_=grp[("p", g)][:].rearrange("p w j -> p (w j)"))

        def xx(g, j):
            nc.scalar.activation(out=junk_a[:], in_=xt[(g, j)][:], func=ACT.Square, accum_out=st_[("nx2", g)][:, j : j + 1])

        def xx_v(g, j):
            nc.vector.scalar_tensor_tensor(out=junk_v[:], in0=xt[(g, j)][:], scalar=1.0, in1=xt[(g, j)][:], op0=ALU.mult, op1=ALU.mult, accum_out=st_[("nx2", g)][:, j : j + 1])

        def nxs(g):
            nc.scalar.activation(out=st_[("nx", g)][:], in_=st_[("nx2", g)][:], func=ACT.Sqrt)

        def inx(g):
            nc.vector.reciprocal(out=st_[("inx", g)][:], in_=st_[("nx", g)][:])
            nc.vector.tensor_tensor(out=st_[("beta", g)][:], in0=sh[:, g, :], in1=st_[("inx", g)][:], op=ALU.mult)
            nc.vector.tensor_tensor(out=st_[("inx2", g)][:], in0=st_[("inx", g)][:], in1=st_[("inx", g)][:], op=ALU.mult)
            nc.vector.tensor_tensor(out=st_[("alpha", g)][:], in0=t0[:, g, :], in1=st_[("inx2", g)][:], op=ALU.mult)

        def bg(g):
            nc.vector.tensor_tensor(out=st_[("bg", g)][:], in0=st_[("beta", g)][:], in1=st_[("gsum", g)][:], op=ALU.mult)

        def qf(g, b0, b1):
            for b in range(b0, b1):
                if b in (0, 3):
                    trp[("s", g, b // 3)] = psum.tile([P, 3 * QN], F32, name="qs", tag="qs", bufs=2)
                if b == 6:
                    trp[("s", g, 2)] = psum.tile([P, 2 * QN], F32, name="th", tag="th", bufs=1)
                for j in range(NJ):
                    nc.tensor.matmul(out=trp[("s", g, b // 3)][:, QN * (b % 3) : QN * (b % 3 + 1)], lhsT=x1[(g, j)][:, P * b : P * (b + 1)], rhs=qt[(g, j)][:, b, 0:QN], start=(j == 0), stop=(j == NJ - 1))

        def qse(g):
            for k in range(2):
                nc.vector.tensor_tensor(out=qs_acc[:, 3 * QN * k : 3 * QN * (k + 1)], in0=trp[("s", g, k)][:], in1=qs_acc[:, 3 * QN * k : 3 * QN * (k + 1)], op=ALU.add)

        def the(g):
            nc.vector.tensor_tensor(out=qs_acc[:, 6 * QN :], in0=trp[("s", g, 2)][:], in1=qs_acc[:, 6 * QN :], op=ALU.add)

        def bcast(vec, nm, tag, bufs):
            for k in range(2):
                trp[(nm, k)] = psum.tile([P, 4, P], F32, name=tag, tag=tag, bufs=bufs)
                for b in range(4):
                    nc.tensor.matmul(out=trp[(nm, k)][:, b, :], lhsT=vec[:, 4 * k + b : 4 * k + b + 1].to_broadcast([P, P]), rhs=ident_f[:], start=True, stop=True)

        def bcast_out(nm, dst):
            for k in range(2):
                nc.vector.tensor_copy(out=dst[:, 512 * k : 512 * (k + 1)], in_=trp[(nm, k)][:].rearrange("p b n -> p (b n)"))

        make_identity(nc, ident_b[:])
        make_identity(nc, ident_f[:])
        nc.vector.memset(a_rows[:], 0.0)
        nc.vector.memset(one[:], 1.0)
        nc.vector.memset(qs_acc[:], 0.0)
        nc.sync.dma_start(out=xn_t[:], in_=xnv)
        nc.sync.dma_start(out=a_rows[0:NB, :], in_=a.rearrange("(b m) -> b m", m=P))
        load_q(0, 0)
        load_q(0, 1)
        for k in range(2):
            nat[("r", k)] = work.tile([P, 4, IN], BF16, name="nat", tag="nat", bufs=2)
            nc.sync.dma_start(out=nat[("r", k)][:], in_=znv[:, 4 * k : 4 * (k + 1), :])
        load_q(0, 2)
        load_q(0, 3)
        for G in range(NGO):
            nat[("z", G)] = work.tile([P, NJ, IN], BF16, name="natz", tag="natz", bufs=2)
            nc.sync.dma_start(out=nat[("z", G)][:], in_=zkv[:, G, :, :])
        for j in range(NJ):
            load_g(0, j)
        for j in range(NJ):
            load_x(0, j)

        nc.scalar.activation(out=ep[:], in_=xn_t[:], func=ACT.Exp, scale=1.0 / SK)
        nc.scalar.activation(out=em[:], in_=xn_t[:], func=ACT.Exp, scale=-1.0 / SK)
        at_ps = psum.tile([P, P], BF16, name="tr", tag="tr", bufs=2)
        nc.tensor.transpose(out=at_ps[:], in_=a_rows[:], identity=ident_b[:])
        nc.vector.tensor_copy(out=a_mb[:], in_=at_ps[:, 0:NB])
        nc.scalar.activation(out=ea[:], in_=a_mb[:], func=ACT.Exp, scale=SK)
        nc.scalar.activation(out=eb[:], in_=a_mb[:], func=ACT.Exp, scale=-SK)
        for b in range(NB):
            rows = nat[("r", b // 4)][:, b % 4, :]
            nc.vector.scalar_tensor_tensor(out=junk_v[:], in0=rows, scalar=1.0, in1=rows, op0=ALU.mult, op1=ALU.mult, accum_out=zn2[:, b : b + 1])
        for j in range(NJ):
            sq(0, j)
            ab(0, j)
            sr(0, j)
            sgn(0, j)
        nc.scalar.activation(out=zn_mb[:], in_=zn2[:], func=ACT.Sqrt)
        nc.vector.tensor_tensor(out=ch[:], in0=ep[:], in1=em[:], op=ALU.add)
        nc.vector.tensor_tensor(out=sh[:], in0=ep[:], in1=em[:], op=ALU.subtract)
        nc.vector.tensor_scalar(out=chn[:], in0=ch[:].unsqueeze(3).to_broadcast([P, NG, NJ, 2]), scalar1=-0.5 * SK, scalar2=None, op0=ALU.mult)
        for j in range(NJ):
            put_ch(0, j)
        nc.vector.tensor_tensor(out=ca_mb[:], in0=ea[:], in1=eb[:], op=ALU.add)
        nc.vector.tensor_tensor(out=sa_mb[:], in0=ea[:], in1=eb[:], op=ALU.subtract)
        nc.vector.tensor_scalar(out=ca_mb[:], in0=ca_mb[:], scalar1=0.5, scalar2=None, op0=ALU.mult)
        nc.vector.tensor_scalar(out=sa_mb[:], in0=sa_mb[:], scalar1=0.5, scalar2=None, op0=ALU.mult)
        bcast(ca_mb, "ca", "acc", 2)
        nc.vector.reciprocal(out=rxn[:], in_=xn_t[:])
        nc.vector.tensor_scalar(out=sh[:], in0=sh[:], scalar1=0.5, scalar2=None, op0=ALU.mult)
        nc.vector.tensor_scalar(out=ch[:], in0=ch[:], scalar1=0.5, scalar2=None, op0=ALU.mult)
        nc.vector.scalar_tensor_tensor(out=lam[:], in0=sh[:], scalar=SK, in1=rxn[:], op0=ALU.mult, op1=ALU.mult)
        nc.vector.reciprocal(out=ilam[:], in_=lam[:])
        nc.vector.tensor_tensor(out=t0[:], in0=ch[:], in1=ilam[:], op=ALU.mult)
        nc.vector.tensor_scalar(out=t0[:], in0=t0[:], scalar1=-1.0, scalar2=None, op0=ALU.add)


        def z_codes(G):
            grp[("z", G)] = work.tile([P, IN, NJ], BF16, name="grp", tag="grp", bufs=1, align_bytes=64)
            interleave(grp[("z", G)], nat[("z", G)])

        def z_quant(G):
            nc.vector.quantize_mx(out=z_c[:, G, :].bitcast(E4), scales=z_s[:, G, :], in_=grp[("z", G)][:].rearrange("p w j -> p (w j)"))

        def epi(g, js):
            for j in js:
                pep(g, j)
            for j in js:
                co(g, j)
            for j in js:
                fi(g, j)

        def m_out(b):
            o1 = work.tile([P, IN], F32, name="y", tag="y", bufs=4)
            for h in range(NH):
                tag, bufs = M_BANKS[(NH * b + h) % len(M_BANKS)]
                macc = psum.tile([P, 512], F32, name=tag, tag=tag, bufs=bufs)
                for g in range(NG):
                    nc.tensor.matmul_mx(out=macc[:], lhsT=ddt_c[:, g, P * b : P * (b + 1)].bitcast(E5), lhsT_scale=ddt_s[:, g, P * b : P * (b + 1)],
                                        rhs=ps_c[:, g, 512 * h : 512 * (h + 1)].bitcast(E4), rhs_scale=ps_s[:, g, 512 * h : 512 * (h + 1)], start=(g == 0), stop=(g == NG - 1))
                nc.vector.scalar_tensor_tensor(out=o1[:, 512 * h : 512 * (h + 1)], in0=nat[("e", b // 4)][:, b % 4, 512 * h : 512 * (h + 1)], scalar=so[:, b : b + 1], in1=macc[:], op0=ALU.mult, op1=ALU.add)
            nc.sync.dma_start(out=o1v[:, b, :], in_=o1[:])

        def load_z(k):
            nat[("e", k)] = work.tile([P, 4, IN], BF16, name="nat", tag="nat", bufs=2)
            nc.sync.dma_start(out=nat[("e", k)][:], in_=znv[:, 4 * k : 4 * (k + 1), :])

        bcast_out("ca", ca_bc)

        for g in range(NG):
            more = g + 1 < NG
            if g > 0:
                for j in range(NJ):
                    sr(g, j)
                nxs(g)
            for b in range(4):
                st(g, b)
            for j in range(NJ):
                ar(g, j)
            if g > 0:
                qse(g - 1)
                epi(g - 1, (2, 3))
                if more:
                    for j in range(NJ):
                        load_x(g + 1, j)
                    load_q(g + 1, 0)
                    put_ch(g + 1, 0)
                    load_g(g + 1, 0)
                the(g - 1)
                inx(g)
            else:
                z_codes(0)
                nc.vector.reciprocal(out=izn[:], in_=zn_mb[:])
                nc.vector.tensor_tensor(out=c_mb[:], in0=sa_mb[:], in1=zn_mb[:], op=ALU.mult)
                bcast(c_mb, "c", "qs", 2)
                z_quant(0)
                z_codes(1)
                for j in range(NJ):
                    load_x(1, j)
                load_q(1, 0)
                put_ch(1, 0)
                load_g(1, 0)
                bcast_out("c", c_bc)
                z_quant(1)
            for j in range(NJ):
                gg(g, j)
            g_t(g, 0)
            for j in range(NJ):
                ps(g, j)
            for b in range(4):
                ln_t(g, b)
                st(g, b + 4)
            for j in range(NJ):
                b_mul(g, j)
            qf(g, 0, 3)
            hs_(g, 0)
            ln_t(g, 4)
            dd_mul(g, 0)
            tr(g, 0)
            hs_(g, 1)
            ln_t(g, 5)
            g_t(g, 1)
            dd_mul(g, 1)
            tr(g, 1)
            dd_mul(g, 2)
            hs_(g, 2)
            ln_t(g, 6)
            dd_mul(g, 3)
            hs_(g, 3)
            ln_t(g, 7)
            g_t(g, 2)
            te(g, 0)
            tr(g, 2)
            te(g, 1)
            tr(g, 3)
            qf(g, 3, 8)
            ip(g)
            hs_(g, 4)
            te(g, 2)
            qo(g, 0)
            hs_(g, 5)
            g_t(g, 3)
            te(g, 3)
            if g == 0:
                for j in range(NJ):
                    xx(0, j)
                nxs(0)
            gs_sum(g, 0)
            qp(g)
            qo(g, 1)
            gs_sum(g, 1)
            it(g)
            hs_(g, 6)
            qo(g, 2)
            gs_sum(g, 2)
            hs_(g, 7)
            qt_(g)
            qo(g, 3)
            gs_sum(g, 3)
            if g == 0:
                inx(0)
            bg(g)
            if more:
                for j in range(NJ):
                    xx(g + 1, j)
            if more:
                for j in range(NJ):
                    mx(g, j)
                    ye(g, j)
            if more:
                for j in range(1, NJ):
                    load_q(g + 1, j)
                    put_ch(g + 1, j)
                for j in range(1, NJ):
                    load_g(g + 1, j)
                for j in range(NJ):
                    sq(g + 1, j)
                for j in range(NJ):
                    ab(g + 1, j)
                for j in range(NJ):
                    sgn(g + 1, j)
                epi(g, (0, 1))

        g = NG - 1
        dg = work.tile([P, NB, P], F32, name="natz", tag="natz", bufs=2)
        s1b = keep.tile([P, NB], F32, name="s1b")
        hs = keep.tile([P, NB], F32, name="hs")
        gz = keep.tile([P, NB], F32, name="gz")
        so = keep.tile([P, NB], F32, name="so")
        sums = qs_acc[:, 0 : NB * QN].rearrange("p (b n) -> p b n", n=QN)
        load_z(0)
        load_z(1)
        qse(g)
        the(g)
        nc.vector.tensor_tensor(out=dg[:], in0=sums[:, :, 0:P], in1=ident_f[:].unsqueeze(1).to_broadcast([P, NB, P]), op=ALU.mult)
        nc.vector.tensor_reduce(out=hs[:], in_=hpart[:].rearrange("p g b -> p b g"), axis=AX.X, op=ALU.add)
        nc.vector.tensor_tensor(out=gz[:], in0=sa_mb[:], in1=sums[:, :, P], op=ALU.mult)
        nc.vector.tensor_reduce(out=s1b[:], in_=dg[:], axis=AX.X, op=ALU.add)
        nc.vector.scalar_tensor_tensor(out=gz[:], in0=hs[:], scalar=2.0 / SK, in1=gz[:], op0=ALU.mult, op1=ALU.add)
        nc.vector.scalar_tensor_tensor(out=gz[:], in0=s1b[:], scalar=-1.0 / SK, in1=gz[:], op0=ALU.mult, op1=ALU.add)
        nc.vector.tensor_tensor(out=so[:], in0=gz[:], in1=izn[:], op=ALU.mult)
        for j in range(NJ):
            mx(g, j)
            ye(g, j)
            m_out(2 * j)
            epi(g, (j,))
            m_out(2 * j + 1)
